import numpy as np
import ml_dtypes


def mxq(x, axis, fmt="e4m3"):
    dtype, down = {"e4m3": (ml_dtypes.float8_e4m3fn, 7), "e5m2": (ml_dtypes.float8_e5m2, 14)}[fmt]
    v = np.moveaxis(np.asarray(x, np.float32).astype(ml_dtypes.bfloat16).astype(np.float64), axis, -1)
    blocks = v.reshape(v.shape[:-1] + (-1, 32))
    amax = np.abs(blocks).max(-1, keepdims=True)
    byte = np.maximum(np.where(amax > 0, np.frexp(amax)[1] - 1 + 127, 0) - down, 1)
    scale = np.exp2(byte - 127.0)
    codes = (blocks / scale).astype(np.float32).astype(dtype).astype(np.float64)
    return np.moveaxis((codes * scale).reshape(v.shape), -1, axis)


WIDE = False


def mx_kscale(k):
    if not WIDE:
        return np.ones(k)
    levels = np.array([10, -10, 5, -5, 0])
    a = np.random.permutation(np.resize(levels, k // 512 * 4)).reshape(k // 512, 4)
    idx = np.arange(k)
    return np.exp2(a[idx // 512, idx % 128 // 32])


BF16 = ml_dtypes.bfloat16


def bf(x):
    return np.asarray(x, np.float32).astype(BF16)


def f64(x):
    return np.asarray(x).astype(np.float64)


B, S, V, C, D = 4, 1024, 32, 128, 1024
EPS_SINK = 0.05
TEMP = 1.0


def l2norm(t):
    n = np.sqrt(np.sum(t * t, axis=1, keepdims=True))
    return t / np.maximum(n, 1e-12)


def sigmoid(v):
    return 1.0 / (1.0 + np.exp(-v))


def setup_inputs():
    s = mx_kscale(S)
    return {"x": bf(np.random.standard_normal((B, S, V)) * s[None, :, None]),
            "cluster_emb": bf(np.random.standard_normal((C, D)) * 3.0),
            "W": bf(np.random.standard_normal((D, S)) * 2.0 / np.sqrt(S) / s[None, :]),
            "b": bf(np.random.standard_normal(D) * 0.5),
            "noise": bf(np.clip(np.random.uniform(size=(V, C)), 0.004, 0.996))}


def reference(x, cluster_emb, W, b, noise):
    x_emb = (mxq(f64(x), 1, "e4m3").transpose(0, 2, 1) @ mxq(f64(W), 1, "e4m3").T) + f64(b)
    xf = x_emb.reshape(-1, D)
    cn = l2norm(f64(cluster_emb))
    prob = (mxq(l2norm(xf), 1, "e4m3") @ mxq(cn, 1, "e4m3").T).reshape(B, V, C)
    prob_avg = np.mean(prob, axis=0)
    Q = np.exp(prob_avg / EPS_SINK)
    prob_avg = Q / np.sum(Q, axis=1, keepdims=True)
    u = f64(noise)
    logit_noise = np.log(u) - np.log(1.0 - u)
    logit_p = np.log(prob_avg + 1e-10) - np.log(1.0 - prob_avg + 1e-10)
    mask = sigmoid((logit_p + logit_noise) / TEMP)
    return prob_avg, mask

@@ -1,0 +1,250 @@
+from contextlib import ExitStack
+
+import concourse.mybir as mybir
+from concourse.masks import make_identity
+
+F32 = mybir.dt.float32
+BF16 = mybir.dt.bfloat16
+U32 = mybir.dt.uint32
+U8 = mybir.dt.uint8
+FP8X4 = mybir.dt.float8_e4m3fn_x4
+ACT = mybir.ActivationFunctionType
+ALU = mybir.AluOpType
+AX = mybir.AxisListType
+
+B, S, V, C, D = 4, 1024, 32, 128, 1024
+P = 128
+PACK = 4
+PAIR = 2
+PASSES = S // (P * PACK)
+ROWS = B * V
+CHUNKS = D // P
+LOAD_CHUNKS = 2
+ROUNDS = CHUNKS // LOAD_CHUNKS
+
+EPS_SINK = 0.05
+EPS_LOG = 1e-10
+INV_NORM_CAP = 1e12
+
+FLOPS = 2 * ROWS * S * D + 2 * ROWS * D * C
+
+
+def tile_cluster_assigner_pa_s_kernel(tc, x, cluster_emb, W, b, noise, out_0, out_1):
+    nc = tc.nc
+    with ExitStack() as ctx:
+        keep = ctx.enter_context(tc.tile_pool(name="keep", bufs=1))
+        stage = ctx.enter_context(tc.tile_pool(name="stage", bufs=2))
+        psum_t = ctx.enter_context(tc.psum_pool(name="psum_t", bufs=4))
+        psum_e = ctx.enter_context(tc.psum_pool(name="psum_e", bufs=2))
+        psum_s = ctx.enter_context(tc.psum_pool(name="psum_s", bufs=2))
+
+        ce_raw = keep.tile([C, D], BF16)
+        nc.sync.dma_start(out=ce_raw[:], in_=cluster_emb)
+        x_raw = keep.tile([P, B, PASSES, PACK, V], BF16)
+        nc.sync.dma_start(
+            out=x_raw[:].rearrange("p n g (u e) v -> p (n g u) (e v)", e=PAIR),
+            in_=x.rearrange("n (g u p e) v -> p (n g u) (e v)", g=PASSES, p=P, e=PAIR),
+        )
+        w_raw = keep.tile([P, CHUNKS, S], BF16)
+        w_rows = W.rearrange("(m j) t -> m j t", j=CHUNKS)
+        for rnd in range(ROUNDS):
+            js = slice(rnd * LOAD_CHUNKS, (rnd + 1) * LOAD_CHUNKS)
+            nc.sync.dma_start(out=w_raw[:, js, :], in_=w_rows[:, js, :])
+        bias_raw = keep.tile([P, CHUNKS], BF16)
+        nc.scalar.dma_start(out=bias_raw[:], in_=b.rearrange("(m j) -> m j", j=CHUNKS))
+        noise_raw = keep.tile([V, C], BF16)
+        nc.scalar.dma_start(out=noise_raw[:], in_=noise)
+
+        ident = keep.tile([P, P], F32)
+        make_identity(nc, ident[:])
+        ones = keep.tile([P, P], F32)
+        nc.vector.memset(ones[:], 1.0)
+        ident_fold = keep.tile([P, V], F32)
+        nc.vector.tensor_reduce(
+            out=ident_fold[:], in_=ident[:].rearrange("p (n v) -> p v n", n=B), axis=AX.X, op=ALU.add
+        )
+        same_v = keep.tile([P, B, V], F32)
+        nc.vector.tensor_copy(out=same_v[:], in_=ident_fold[:].unsqueeze(1).to_broadcast([P, B, V]))
+        table_in = keep.tile([P, 1], F32)
+        nc.vector.memset(table_in[:], 1.0)
+        table_out = keep.tile([P, 1], F32)
+        nc.scalar.activation(out=table_out[:], in_=table_in[:], func=ACT.Abs_reciprocal_sqrt)
+
+        bias = keep.tile([P, CHUNKS], F32)
+        nc.vector.tensor_copy(out=bias[:], in_=bias_raw[:])
+        u_on = keep.tile([V, C], F32)
+        nc.vector.tensor_copy(out=u_on[:], in_=noise_raw[:])
+        u_off = keep.tile([V, C], F32)
+        nc.vector.tensor_scalar(
+            out=u_off[:], in0=noise_raw[:], scalar1=-1.0, scalar2=1.0, op0=ALU.mult, op1=ALU.add
+        )
+
+        x_grouped = keep.tile([P, PASSES, ROWS, PACK], BF16, align_bytes=64)
+        for g in range(PASSES):
+            nc.vector.tensor_copy(
+                out=x_grouped[:, g].rearrange("p (n v) i -> p n v i", n=B),
+                in_=x_raw[:, :, g].rearrange("p n i v -> p n v i"),
+            )
+        x_codes = keep.tile([P, PASSES, ROWS], U32, align_bytes=64)
+        x_scales = keep.tile([P, PASSES, ROWS], U8, align_bytes=64)
+        nc.vector.quantize_mx(
+            out=x_codes[:].rearrange("p g r -> p (g r)").bitcast(FP8X4),
+            scales=x_scales[:].rearrange("p g r -> p (g r)"),
+            in_=x_grouped[:].rearrange("p g r i -> p (g r i)"),
+        )
+
+        ce_sq = keep.tile([C, D], BF16)
+        ce_ss = keep.tile([C, 1], F32)
+        nc.scalar.activation(out=ce_sq[:], in_=ce_raw[:], func=ACT.Square, accum_out=ce_ss[:])
+        ce_rnorm = keep.tile([C, 1], F32)
+        nc.scalar.activation(out=ce_rnorm[:], in_=ce_ss[:], func=ACT.Abs_reciprocal_sqrt)
+        ce_scale = keep.tile([C, 1], F32)
+        nc.vector.tensor_scalar_min(out=ce_scale[:], in0=ce_rnorm[:], scalar1=INV_NORM_CAP)
+        cn_f32 = keep.tile([C, CHUNKS, P], F32)
+        nc.scalar.activation(
+            out=cn_f32[:],
+            in_=ce_raw[:].rearrange("c (m j) -> c j m", j=CHUNKS),
+            func=ACT.Copy,
+            scale=ce_scale[:, 0:1],
+        )
+        cn_grouped = keep.tile([P, PASSES, C, PACK], BF16, align_bytes=64)
+        for g in range(PASSES):
+            cn_t = psum_t.tile([P, PACK, P], F32, tag="transposed")
+            for i in range(PACK):
+                nc.tensor.transpose(cn_t[:, i, :], cn_f32[:, PACK * g + i, :], ident[:])
+            nc.scalar.copy(out=cn_grouped[:, g], in_=cn_t[:].rearrange("m i c -> m c i"))
+        cn_codes = keep.tile([P, PASSES, C], U32, align_bytes=64)
+        cn_scales = keep.tile([P, PASSES, C], U8, align_bytes=64)
+        nc.vector.quantize_mx(
+            out=cn_codes[:].rearrange("p g c -> p (g c)").bitcast(FP8X4),
+            scales=cn_scales[:].rearrange("p g c -> p (g c)"),
+            in_=cn_grouped[:].rearrange("p g c i -> p (g c i)"),
+        )
+
+        w_words = w_raw[:].rearrange("m j t -> m (j t)").bitcast(F32)
+        words_per_chunk = S // PAIR
+        w_codes = keep.tile([P, CHUNKS, PASSES, P], U32, align_bytes=64)
+        w_scales = keep.tile([P, CHUNKS, PASSES, P], U8, align_bytes=64)
+        emb = keep.tile([P, CHUNKS, ROWS], F32)
+        ss_ps = psum_s.tile([P, ROWS], F32, tag="small")
+        for rnd in range(ROUNDS):
+            js = slice(rnd * LOAD_CHUNKS, (rnd + 1) * LOAD_CHUNKS)
+            w_grouped = stage.tile([P, LOAD_CHUNKS, PASSES, P, PACK], BF16, align_bytes=64)
+            for k in range(LOAD_CHUNKS):
+                j = rnd * LOAD_CHUNKS + k
+                w_t = psum_t.tile([P, PACK, P], F32, tag="transposed")
+                for a in range(PACK):
+                    first = j * words_per_chunk + a * P
+                    nc.tensor.transpose(w_t[:, a, :], w_words[:, first : first + P], ident[:])
+                copy_out = nc.scalar.copy if k % 2 == 0 else nc.vector.tensor_copy
+                copy_out(
+                    out=w_grouped[:, k]
+                    .rearrange("p g m i -> p (g m i)")
+                    .bitcast(F32)
+                    .rearrange("p (g m u) -> p g m u", g=PASSES, u=PAIR),
+                    in_=w_t[:].rearrange("p (g u) m -> p g m u", g=PASSES),
+                )
+            nc.vector.quantize_mx(
+                out=w_codes[:, js].rearrange("p j g m -> p (j g m)").bitcast(FP8X4),
+                scales=w_scales[:, js].rearrange("p j g m -> p (j g m)"),
+                in_=w_grouped[:].rearrange("p j g m i -> p (j g m i)"),
+            )
+            emb_ps = psum_e.tile([P, LOAD_CHUNKS, ROWS], F32)
+            for k in range(LOAD_CHUNKS):
+                j = rnd * LOAD_CHUNKS + k
+                for g in range(PASSES):
+                    nc.tensor.matmul_mx(
+                        out=emb_ps[:, k, :],
+                        lhsT=w_codes[:, j, g, :].bitcast(FP8X4),
+                        lhsT_scale=w_scales[:, j, g, :],
+                        rhs=x_codes[:, g, :].bitcast(FP8X4),
+                        rhs_scale=x_scales[:, g, :],
+                        start=(g == 0),
+                        stop=(g == PASSES - 1),
+                    )
+            emb_sq = stage.tile([P, LOAD_CHUNKS, ROWS], F32)
+            for k in range(LOAD_CHUNKS):
+                j = rnd * LOAD_CHUNKS + k
+                nc.scalar.activation(
+                    out=emb_sq[:, k, :], in_=emb_ps[:, k, :], func=ACT.Square, bias=bias[:, j : j + 1]
+                )
+            for k in range(LOAD_CHUNKS):
+                j = rnd * LOAD_CHUNKS + k
+                nc.scalar.activation(
+                    out=emb[:, j, :], in_=emb_ps[:, k, :], func=ACT.Identity, bias=bias[:, j : j + 1]
+                )
+            sq_round = stage.tile([P, ROWS], F32)
+            nc.vector.tensor_add(out=sq_round[:], in0=emb_sq[:, 0, :], in1=emb_sq[:, 1, :])
+            nc.tensor.matmul(
+                out=ss_ps[:], lhsT=ones[:], rhs=sq_round[:], start=(rnd == 0), stop=(rnd == ROUNDS - 1)
+            )
+
+        rnorm = keep.tile([P, ROWS], F32)
+        nc.scalar.activation(out=rnorm[:], in_=ss_ps[:], func=ACT.Abs_reciprocal_sqrt)
+        nc.scalar.activation(out=table_out[:], in_=rnorm[:, 0:1], func=ACT.Exp)
+        xn_grouped = keep.tile([P, PASSES, ROWS, PACK], BF16, align_bytes=64)
+        for g in range(PASSES):
+            nc.vector.scalar_tensor_tensor(
+                out=xn_grouped[:, g],
+                in0=rnorm[:].unsqueeze(2).to_broadcast([P, ROWS, PACK]),
+                scalar=INV_NORM_CAP,
+                in1=emb[:, PACK * g : PACK * (g + 1), :].rearrange("m i r -> m r i"),
+                op0=ALU.min,
+                op1=ALU.mult,
+            )
+        xn_codes = keep.tile([P, PASSES, ROWS], U32, align_bytes=64)
+        xn_scales = keep.tile([P, PASSES, ROWS], U8, align_bytes=64)
+        nc.vector.quantize_mx(
+            out=xn_codes[:].rearrange("p g r -> p (g r)").bitcast(FP8X4),
+            scales=xn_scales[:].rearrange("p g r -> p (g r)"),
+            in_=xn_grouped[:].rearrange("p g r i -> p (g r i)"),
+        )
+
+        prob_ps = psum_s.tile([ROWS, C], F32, tag="small")
+        for g in range(PASSES):
+            nc.tensor.matmul_mx(
+                out=prob_ps[:],
+                lhsT=xn_codes[:, g, :].bitcast(FP8X4),
+                lhsT_scale=xn_scales[:, g, :],
+                rhs=cn_codes[:, g, :].bitcast(FP8X4),
+                rhs_scale=cn_scales[:, g, :],
+                start=(g == 0),
+                stop=(g == PASSES - 1),
+            )
+        prob = keep.tile([ROWS, C], F32)
+        nc.vector.tensor_copy(out=prob[:], in_=prob_ps[:])
+        batch_sum_ps = psum_s.tile([ROWS, C], F32, tag="small")
+        nc.tensor.matmul(
+            out=batch_sum_ps[:], lhsT=same_v[:].rearrange("p n v -> p (n v)"), rhs=prob[:], start=True, stop=True
+        )
+
+        q_exp = keep.tile([V, C], F32)
+        q_sum = keep.tile([V, 1], F32)
+        nc.scalar.activation(
+            out=q_exp[:], in_=batch_sum_ps[0:V, :], func=ACT.Exp, scale=1.0 / (B * EPS_SINK), accum_out=q_sum[:]
+        )
+        q_rsum = keep.tile([V, 1], F32)
+        nc.vector.reciprocal(out=q_rsum[:], in_=q_sum[:])
+        prob_avg = keep.tile([V, C], F32)
+        nc.vector.tensor_scalar_mul(out=prob_avg[:], in0=q_exp[:], scalar1=q_rsum[:, 0:1])
+        nc.sync.dma_start(out=out_0, in_=prob_avg[:])
+
+        on = keep.tile([V, C], F32)
+        nc.vector.scalar_tensor_tensor(
+            out=on[:], in0=prob_avg[:], scalar=EPS_LOG, in1=u_on[:], op0=ALU.add, op1=ALU.mult
+        )
+        rest = keep.tile([V, C], F32)
+        nc.vector.tensor_scalar(
+            out=rest[:], in0=prob_avg[:], scalar1=-1.0, scalar2=1.0, op0=ALU.mult, op1=ALU.add
+        )
+        off = keep.tile([V, C], F32)
+        nc.vector.scalar_tensor_tensor(
+            out=off[:], in0=rest[:], scalar=EPS_LOG, in1=u_off[:], op0=ALU.add, op1=ALU.mult
+        )
+        both = keep.tile([V, C], F32)
+        nc.vector.tensor_add(out=both[:], in0=on[:], in1=off[:])
+        rboth = keep.tile([V, C], F32)
+        nc.vector.reciprocal(out=rboth[:], in_=both[:])
+        mask = keep.tile([V, C], F32)
+        nc.vector.tensor_mul(out=mask[:], in0=on[:], in1=rboth[:])
+        nc.sync.dma_start(out=out_1, in_=mask[:])

@@ -38,6 +38,8 @@ def tile_cluster_assigner_pa_s_kernel(tc, x, cluster_emb, W, b, noise, out_0, ou
         psum_e = ctx.enter_context(tc.psum_pool(name="psum_e", bufs=2))
         psum_s = ctx.enter_context(tc.psum_pool(name="psum_s", bufs=2))
 
+        ctx.enter_context(tc.manual_schedule())
+
         ce_raw = keep.tile([C, D], BF16)
         nc.sync.dma_start(out=ce_raw[:], in_=cluster_emb)
         x_raw = keep.tile([P, B, PASSES, PACK, V], BF16)
@@ -59,45 +61,28 @@ def tile_cluster_assigner_pa_s_kernel(tc, x, cluster_emb, W, b, noise, out_0, ou
         make_identity(nc, ident[:])
         ones = keep.tile([P, P], F32)
         nc.vector.memset(ones[:], 1.0)
+        table_in = keep.tile([P, 1], F32)
+        nc.vector.memset(table_in[:], 1.0)
+        table_out = keep.tile([P, 1], F32)
+        nc.scalar.activation(out=table_out[:], in_=table_in[:], func=ACT.Abs_reciprocal_sqrt)
         ident_fold = keep.tile([P, V], F32)
         nc.vector.tensor_reduce(
             out=ident_fold[:], in_=ident[:].rearrange("p (n v) -> p v n", n=B), axis=AX.X, op=ALU.add
         )
         same_v = keep.tile([P, B, V], F32)
         nc.vector.tensor_copy(out=same_v[:], in_=ident_fold[:].unsqueeze(1).to_broadcast([P, B, V]))
-        table_in = keep.tile([P, 1], F32)
-        nc.vector.memset(table_in[:], 1.0)
-        table_out = keep.tile([P, 1], F32)
-        nc.scalar.activation(out=table_out[:], in_=table_in[:], func=ACT.Abs_reciprocal_sqrt)
-
-        bias = keep.tile([P, CHUNKS], F32)
-        nc.vector.tensor_copy(out=bias[:], in_=bias_raw[:])
-        u_on = keep.tile([V, C], F32)
-        nc.vector.tensor_copy(out=u_on[:], in_=noise_raw[:])
-        u_off = keep.tile([V, C], F32)
-        nc.vector.tensor_scalar(
-            out=u_off[:], in0=noise_raw[:], scalar1=-1.0, scalar2=1.0, op0=ALU.mult, op1=ALU.add
-        )
-
-        x_grouped = keep.tile([P, PASSES, ROWS, PACK], BF16, align_bytes=64)
-        for g in range(PASSES):
-            nc.vector.tensor_copy(
-                out=x_grouped[:, g].rearrange("p (n v) i -> p n v i", n=B),
-                in_=x_raw[:, :, g].rearrange("p n i v -> p n v i"),
-            )
-        x_codes = keep.tile([P, PASSES, ROWS], U32, align_bytes=64)
-        x_scales = keep.tile([P, PASSES, ROWS], U8, align_bytes=64)
-        nc.vector.quantize_mx(
-            out=x_codes[:].rearrange("p g r -> p (g r)").bitcast(FP8X4),
-            scales=x_scales[:].rearrange("p g r -> p (g r)"),
-            in_=x_grouped[:].rearrange("p g r i -> p (g r i)"),
-        )
 
         ce_sq = keep.tile([C, D], BF16)
         ce_ss = keep.tile([C, 1], F32)
         nc.scalar.activation(out=ce_sq[:], in_=ce_raw[:], func=ACT.Square, accum_out=ce_ss[:])
         ce_rnorm = keep.tile([C, 1], F32)
         nc.scalar.activation(out=ce_rnorm[:], in_=ce_ss[:], func=ACT.Abs_reciprocal_sqrt)
+        x_grouped = keep.tile([P, PASSES, ROWS, PACK], BF16, align_bytes=64)
+        for g in range(PASSES):
+            nc.vector.tensor_copy(
+                out=x_grouped[:, g].rearrange("p (n v) i -> p n v i", n=B),
+                in_=x_raw[:, :, g].rearrange("p n i v -> p n v i"),
+            )
         ce_scale = keep.tile([C, 1], F32)
         nc.vector.tensor_scalar_min(out=ce_scale[:], in0=ce_rnorm[:], scalar1=INV_NORM_CAP)
         cn_f32 = keep.tile([C, CHUNKS, P], F32)
@@ -107,32 +92,31 @@ def tile_cluster_assigner_pa_s_kernel(tc, x, cluster_emb, W, b, noise, out_0, ou
             func=ACT.Copy,
             scale=ce_scale[:, 0:1],
         )
-        cn_grouped = keep.tile([P, PASSES, C, PACK], BF16, align_bytes=64)
-        for g in range(PASSES):
-            cn_t = psum_t.tile([P, PACK, P], F32, tag="transposed")
-            for i in range(PACK):
-                nc.tensor.transpose(cn_t[:, i, :], cn_f32[:, PACK * g + i, :], ident[:])
-            nc.scalar.copy(out=cn_grouped[:, g], in_=cn_t[:].rearrange("m i c -> m c i"))
-        cn_codes = keep.tile([P, PASSES, C], U32, align_bytes=64)
-        cn_scales = keep.tile([P, PASSES, C], U8, align_bytes=64)
+        x_codes = keep.tile([P, PASSES, ROWS], U32, align_bytes=64)
+        x_scales = keep.tile([P, PASSES, ROWS], U8, align_bytes=64)
         nc.vector.quantize_mx(
-            out=cn_codes[:].rearrange("p g c -> p (g c)").bitcast(FP8X4),
-            scales=cn_scales[:].rearrange("p g c -> p (g c)"),
-            in_=cn_grouped[:].rearrange("p g c i -> p (g c i)"),
+            out=x_codes[:].rearrange("p g r -> p (g r)").bitcast(FP8X4),
+            scales=x_scales[:].rearrange("p g r -> p (g r)"),
+            in_=x_grouped[:].rearrange("p g r i -> p (g r i)"),
         )
+        bias = keep.tile([P, CHUNKS], F32)
+        nc.vector.tensor_copy(out=bias[:], in_=bias_raw[:])
 
         w_words = w_raw[:].rearrange("m j t -> m (j t)").bitcast(F32)
         words_per_chunk = S // PAIR
         w_codes = keep.tile([P, CHUNKS, PASSES, P], U32, align_bytes=64)
         w_scales = keep.tile([P, CHUNKS, PASSES, P], U8, align_bytes=64)
         emb = keep.tile([P, CHUNKS, ROWS], F32)
-        ss_ps = psum_s.tile([P, ROWS], F32, tag="small")
-        for rnd in range(ROUNDS):
-            js = slice(rnd * LOAD_CHUNKS, (rnd + 1) * LOAD_CHUNKS)
+        w_grouped_of = {}
+        emb_ps_of = {}
+        sq_round_of = {}
+
+        def transpose_w(rnd):
             w_grouped = stage.tile([P, LOAD_CHUNKS, PASSES, P, PACK], BF16, align_bytes=64)
+            w_grouped_of[rnd] = w_grouped
             for k in range(LOAD_CHUNKS):
                 j = rnd * LOAD_CHUNKS + k
-                w_t = psum_t.tile([P, PACK, P], F32, tag="transposed")
+                w_t = psum_t.tile([P, PACK, P], F32)
                 for a in range(PACK):
                     first = j * words_per_chunk + a * P
                     nc.tensor.transpose(w_t[:, a, :], w_words[:, first : first + P], ident[:])
@@ -144,12 +128,18 @@ def tile_cluster_assigner_pa_s_kernel(tc, x, cluster_emb, W, b, noise, out_0, ou
                     .rearrange("p (g m u) -> p g m u", g=PASSES, u=PAIR),
                     in_=w_t[:].rearrange("p (g u) m -> p g m u", g=PASSES),
                 )
+
+        def quantise_w(rnd):
+            js = slice(rnd * LOAD_CHUNKS, (rnd + 1) * LOAD_CHUNKS)
             nc.vector.quantize_mx(
                 out=w_codes[:, js].rearrange("p j g m -> p (j g m)").bitcast(FP8X4),
                 scales=w_scales[:, js].rearrange("p j g m -> p (j g m)"),
-                in_=w_grouped[:].rearrange("p j g m i -> p (j g m i)"),
+                in_=w_grouped_of[rnd][:].rearrange("p j g m i -> p (j g m i)"),
             )
+
+        def multiply_w_x(rnd):
             emb_ps = psum_e.tile([P, LOAD_CHUNKS, ROWS], F32)
+            emb_ps_of[rnd] = emb_ps
             for k in range(LOAD_CHUNKS):
                 j = rnd * LOAD_CHUNKS + k
                 for g in range(PASSES):
@@ -162,6 +152,9 @@ def tile_cluster_assigner_pa_s_kernel(tc, x, cluster_emb, W, b, noise, out_0, ou
                         start=(g == 0),
                         stop=(g == PASSES - 1),
                     )
+
+        def add_bias_and_square(rnd):
+            emb_ps = emb_ps_of[rnd]
             emb_sq = stage.tile([P, LOAD_CHUNKS, ROWS], F32)
             for k in range(LOAD_CHUNKS):
                 j = rnd * LOAD_CHUNKS + k
@@ -174,10 +167,47 @@ def tile_cluster_assigner_pa_s_kernel(tc, x, cluster_emb, W, b, noise, out_0, ou
                     out=emb[:, j, :], in_=emb_ps[:, k, :], func=ACT.Identity, bias=bias[:, j : j + 1]
                 )
             sq_round = stage.tile([P, ROWS], F32)
+            sq_round_of[rnd] = sq_round
             nc.vector.tensor_add(out=sq_round[:], in0=emb_sq[:, 0, :], in1=emb_sq[:, 1, :])
-            nc.tensor.matmul(
-                out=ss_ps[:], lhsT=ones[:], rhs=sq_round[:], start=(rnd == 0), stop=(rnd == ROUNDS - 1)
-            )
+
+        transpose_w(0)
+        quantise_w(0)
+        cn_grouped = keep.tile([P, PASSES, C, PACK], BF16, align_bytes=64)
+        for g in range(PASSES):
+            cn_t = psum_s.tile([P, PACK, P], F32, tag="small")
+            for i in range(PACK):
+                nc.tensor.transpose(cn_t[:, i, :], cn_f32[:, PACK * g + i, :], ident[:])
+            copy_out = nc.scalar.copy if g % 2 == 0 else nc.vector.tensor_copy
+            copy_out(out=cn_grouped[:, g], in_=cn_t[:].rearrange("m i c -> m c i"))
+
+        ss_ps = psum_s.tile([P, ROWS], F32, tag="small")
+        for s in range(1, ROUNDS + 2):
+            if s >= 2:
+                add_bias_and_square(s - 2)
+            if s < ROUNDS:
+                transpose_w(s)
+            if s >= 2:
+                nc.tensor.matmul(
+                    out=ss_ps[:], lhsT=ones[:], rhs=sq_round_of[s - 2][:], start=(s == 2), stop=(s == ROUNDS + 1)
+                )
+            if s < ROUNDS:
+                quantise_w(s)
+            if s <= ROUNDS:
+                multiply_w_x(s - 1)
+
+        cn_codes = keep.tile([P, PASSES, C], U32, align_bytes=64)
+        cn_scales = keep.tile([P, PASSES, C], U8, align_bytes=64)
+        nc.vector.quantize_mx(
+            out=cn_codes[:].rearrange("p g c -> p (g c)").bitcast(FP8X4),
+            scales=cn_scales[:].rearrange("p g c -> p (g c)"),
+            in_=cn_grouped[:].rearrange("p g c i -> p (g c i)"),
+        )
+        u_on = keep.tile([V, C], F32)
+        nc.vector.tensor_copy(out=u_on[:], in_=noise_raw[:])
+        u_off = keep.tile([V, C], F32)
+        nc.vector.tensor_scalar(
+            out=u_off[:], in0=noise_raw[:], scalar1=-1.0, scalar2=1.0, op0=ALU.mult, op1=ALU.add
+        )
 
         rnorm = keep.tile([P, ROWS], F32)
         nc.scalar.activation(out=rnorm[:], in_=ss_ps[:], func=ACT.Abs_reciprocal_sqrt)

@@ -7,6 +7,7 @@ F32 = mybir.dt.float32
 BF16 = mybir.dt.bfloat16
 U32 = mybir.dt.uint32
 U8 = mybir.dt.uint8
+I32 = mybir.dt.int32
 FP8X4 = mybir.dt.float8_e4m3fn_x4
 ACT = mybir.ActivationFunctionType
 ALU = mybir.AluOpType
@@ -21,6 +22,7 @@ ROWS = B * V
 CHUNKS = D // P
 LOAD_CHUNKS = 2
 ROUNDS = CHUNKS // LOAD_CHUNKS
+WARM_PASSES = 32
 
 EPS_SINK = 0.05
 EPS_LOG = 1e-10
@@ -57,6 +59,23 @@ def tile_cluster_assigner_pa_s_kernel(tc, x, cluster_emb, W, b, noise, out_0, ou
         noise_raw = keep.tile([V, C], BF16)
         nc.scalar.dma_start(out=noise_raw[:], in_=noise)
 
+        zeros = keep.tile([P, P * PACK], BF16, align_bytes=64)
+        nc.vector.memset(zeros[:].bitcast(I32), 0)
+        zero_codes = keep.tile([P, P], U32, align_bytes=64)
+        zero_scales = keep.tile([P, P], U8, align_bytes=64)
+        nc.vector.quantize_mx(out=zero_codes[:].bitcast(FP8X4), scales=zero_scales[:], in_=zeros[:])
+        warm_ps = psum_e.tile([P, P], F32, tag="emb_ps")
+        for idle_pass in range(WARM_PASSES):
+            nc.tensor.matmul_mx(
+                out=warm_ps[:],
+                lhsT=zero_codes[:].bitcast(FP8X4),
+                lhsT_scale=zero_scales[:],
+                rhs=zero_codes[:].bitcast(FP8X4),
+                rhs_scale=zero_scales[:],
+                start=True,
+                stop=True,
+            )
+
         ident = keep.tile([P, P], F32)
         make_identity(nc, ident[:])
         ones = keep.tile([P, P], F32)
@@ -72,6 +91,10 @@ def tile_cluster_assigner_pa_s_kernel(tc, x, cluster_emb, W, b, noise, out_0, ou
         same_v = keep.tile([P, B, V], F32)
         nc.vector.tensor_copy(out=same_v[:], in_=ident_fold[:].unsqueeze(1).to_broadcast([P, B, V]))
 
+        ce_t = psum_s.tile([P, CHUNKS // PAIR, C], F32, tag="small")
+        ce_words = ce_raw[:].bitcast(F32).rearrange("c (m w) -> c w m", w=CHUNKS // PAIR)
+        for w in range(CHUNKS // PAIR):
+            nc.tensor.transpose(ce_t[:, w, :], ce_words[:, w, :], ident[:])
         ce_sq = keep.tile([C, D], BF16)
         ce_ss = keep.tile([C, 1], F32)
         nc.scalar.activation(out=ce_sq[:], in_=ce_raw[:], func=ACT.Square, accum_out=ce_ss[:])
@@ -85,13 +108,6 @@ def tile_cluster_assigner_pa_s_kernel(tc, x, cluster_emb, W, b, noise, out_0, ou
             )
         ce_scale = keep.tile([C, 1], F32)
         nc.vector.tensor_scalar_min(out=ce_scale[:], in0=ce_rnorm[:], scalar1=INV_NORM_CAP)
-        cn_f32 = keep.tile([C, CHUNKS, P], F32)
-        nc.scalar.activation(
-            out=cn_f32[:],
-            in_=ce_raw[:].rearrange("c (m j) -> c j m", j=CHUNKS),
-            func=ACT.Copy,
-            scale=ce_scale[:, 0:1],
-        )
         x_codes = keep.tile([P, PASSES, ROWS], U32, align_bytes=64)
         x_scales = keep.tile([P, PASSES, ROWS], U8, align_bytes=64)
         nc.vector.quantize_mx(
@@ -101,6 +117,20 @@ def tile_cluster_assigner_pa_s_kernel(tc, x, cluster_emb, W, b, noise, out_0, ou
         )
         bias = keep.tile([P, CHUNKS], F32)
         nc.vector.tensor_copy(out=bias[:], in_=bias_raw[:])
+        u_on = keep.tile([V, C], F32)
+        nc.vector.tensor_copy(out=u_on[:], in_=noise_raw[:])
+        u_on_eps = keep.tile([V, C], F32)
+        nc.vector.tensor_scalar_mul(out=u_on_eps[:], in0=noise_raw[:], scalar1=EPS_LOG)
+        u_diff = keep.tile([V, C], F32)
+        nc.vector.tensor_scalar(
+            out=u_diff[:], in0=noise_raw[:], scalar1=2.0, scalar2=-1.0, op0=ALU.mult, op1=ALU.add
+        )
+        u_off = keep.tile([V, C], F32)
+        nc.vector.tensor_scalar(
+            out=u_off[:], in0=noise_raw[:], scalar1=-1.0, scalar2=1.0, op0=ALU.mult, op1=ALU.add
+        )
+        u_off_eps = keep.tile([V, C], F32)
+        nc.vector.tensor_scalar_add(out=u_off_eps[:], in0=u_off[:], scalar1=EPS_LOG)
 
         w_words = w_raw[:].rearrange("m j t -> m (j t)").bitcast(F32)
         words_per_chunk = S // PAIR
@@ -109,7 +139,7 @@ def tile_cluster_assigner_pa_s_kernel(tc, x, cluster_emb, W, b, noise, out_0, ou
         emb = keep.tile([P, CHUNKS, ROWS], F32)
         w_grouped_of = {}
         emb_ps_of = {}
-        sq_round_of = {}
+        sq_round = keep.tile([P, ROUNDS, ROWS], F32)
 
         def transpose_w(rnd):
             w_grouped = stage.tile([P, LOAD_CHUNKS, PASSES, P, PACK], BF16, align_bytes=64)
@@ -166,47 +196,51 @@ def tile_cluster_assigner_pa_s_kernel(tc, x, cluster_emb, W, b, noise, out_0, ou
                 nc.scalar.activation(
                     out=emb[:, j, :], in_=emb_ps[:, k, :], func=ACT.Identity, bias=bias[:, j : j + 1]
                 )
-            sq_round = stage.tile([P, ROWS], F32)
-            sq_round_of[rnd] = sq_round
-            nc.vector.tensor_add(out=sq_round[:], in0=emb_sq[:, 0, :], in1=emb_sq[:, 1, :])
+            nc.vector.tensor_add(out=sq_round[:, rnd, :], in0=emb_sq[:, 0, :], in1=emb_sq[:, 1, :])
 
-        transpose_w(0)
-        quantise_w(0)
-        cn_grouped = keep.tile([P, PASSES, C, PACK], BF16, align_bytes=64)
-        for g in range(PASSES):
-            cn_t = psum_s.tile([P, PACK, P], F32, tag="small")
-            for i in range(PACK):
-                nc.tensor.transpose(cn_t[:, i, :], cn_f32[:, PACK * g + i, :], ident[:])
-            copy_out = nc.scalar.copy if g % 2 == 0 else nc.vector.tensor_copy
-            copy_out(out=cn_grouped[:, g], in_=cn_t[:].rearrange("m i c -> m c i"))
+        def add_to_norms(rnd):
+            nc.tensor.matmul(
+                out=ss_ps[:], lhsT=ones[:], rhs=sq_round[:, rnd, :], start=(rnd == 0), stop=(rnd == ROUNDS - 1)
+            )
 
-        ss_ps = psum_s.tile([P, ROWS], F32, tag="small")
-        for s in range(1, ROUNDS + 2):
-            if s >= 2:
-                add_bias_and_square(s - 2)
+        def pipeline_step(s):
             if s < ROUNDS:
                 transpose_w(s)
-            if s >= 2:
-                nc.tensor.matmul(
-                    out=ss_ps[:], lhsT=ones[:], rhs=sq_round_of[s - 2][:], start=(s == 2), stop=(s == ROUNDS + 1)
-                )
-            if s < ROUNDS:
                 quantise_w(s)
-            if s <= ROUNDS:
-                multiply_w_x(s - 1)
+            if 2 <= s < ROUNDS + 2:
+                multiply_w_x(s - 2)
+            if s >= 3:
+                add_bias_and_square(s - 3)
 
+        pipeline_step(0)
+        scale_ps = psum_s.tile([P, C], F32, tag="small")
+        nc.tensor.matmul(
+            out=scale_ps[:], lhsT=ce_scale[:, 0:1].to_broadcast([C, P]), rhs=ident[:], start=True, stop=True
+        )
+        cn_scale = keep.tile([P, C], F32)
+        nc.scalar.copy(out=cn_scale[:], in_=scale_ps[:])
+        for s in range(1, ROUNDS + 3):
+            pipeline_step(s)
+        ss_ps = psum_s.tile([P, ROWS], F32, tag="small")
+        for rnd in range(ROUNDS - 1):
+            add_to_norms(rnd)
+
+        add_to_norms(ROUNDS - 1)
+
+        cn_grouped = keep.tile([P, PASSES, C, PACK], BF16, align_bytes=64)
+        for g in range(PASSES):
+            nc.vector.tensor_tensor(
+                out=cn_grouped[:, g].rearrange("m c (u e) -> m c u e", e=PAIR),
+                in0=ce_t[:, PAIR * g : PAIR * (g + 1), :].bitcast(BF16).rearrange("m u (c e) -> m c u e", e=PAIR),
+                in1=cn_scale[:].unsqueeze(2).unsqueeze(3).to_broadcast([P, C, PAIR, PAIR]),
+                op=ALU.mult,
+            )
         cn_codes = keep.tile([P, PASSES, C], U32, align_bytes=64)
         cn_scales = keep.tile([P, PASSES, C], U8, align_bytes=64)
         nc.vector.quantize_mx(
             out=cn_codes[:].rearrange("p g c -> p (g c)").bitcast(FP8X4),
             scales=cn_scales[:].rearrange("p g c -> p (g c)"),
             in_=cn_grouped[:].rearrange("p g c i -> p (g c i)"),
-        )
-        u_on = keep.tile([V, C], F32)
-        nc.vector.tensor_copy(out=u_on[:], in_=noise_raw[:])
-        u_off = keep.tile([V, C], F32)
-        nc.vector.tensor_scalar(
-            out=u_off[:], in0=noise_raw[:], scalar1=-1.0, scalar2=1.0, op0=ALU.mult, op1=ALU.add
         )
 
         rnorm = keep.tile([P, ROWS], F32)
@@ -253,28 +287,25 @@ def tile_cluster_assigner_pa_s_kernel(tc, x, cluster_emb, W, b, noise, out_0, ou
         nc.scalar.activation(
             out=q_exp[:], in_=batch_sum_ps[0:V, :], func=ACT.Exp, scale=1.0 / (B * EPS_SINK), accum_out=q_sum[:]
         )
+        q_diff = keep.tile([V, C], F32)
+        nc.vector.tensor_mul(out=q_diff[:], in0=q_exp[:], in1=u_diff[:])
+        q_on = keep.tile([V, C], F32)
+        nc.vector.tensor_mul(out=q_on[:], in0=q_exp[:], in1=u_on[:])
+        both = keep.tile([V, C], F32)
+        nc.vector.scalar_tensor_tensor(
+            out=both[:], in0=u_off_eps[:], scalar=q_sum[:, 0:1], in1=q_diff[:], op0=ALU.mult, op1=ALU.add
+        )
         q_rsum = keep.tile([V, 1], F32)
         nc.vector.reciprocal(out=q_rsum[:], in_=q_sum[:])
-        prob_avg = keep.tile([V, C], F32)
-        nc.vector.tensor_scalar_mul(out=prob_avg[:], in0=q_exp[:], scalar1=q_rsum[:, 0:1])
-        nc.sync.dma_start(out=out_0, in_=prob_avg[:])
-
         on = keep.tile([V, C], F32)
         nc.vector.scalar_tensor_tensor(
-            out=on[:], in0=prob_avg[:], scalar=EPS_LOG, in1=u_on[:], op0=ALU.add, op1=ALU.mult
+            out=on[:], in0=u_on_eps[:], scalar=q_sum[:, 0:1], in1=q_on[:], op0=ALU.mult, op1=ALU.add
         )
-        rest = keep.tile([V, C], F32)
-        nc.vector.tensor_scalar(
-            out=rest[:], in0=prob_avg[:], scalar1=-1.0, scalar2=1.0, op0=ALU.mult, op1=ALU.add
-        )
-        off = keep.tile([V, C], F32)
-        nc.vector.scalar_tensor_tensor(
-            out=off[:], in0=rest[:], scalar=EPS_LOG, in1=u_off[:], op0=ALU.add, op1=ALU.mult
-        )
-        both = keep.tile([V, C], F32)
-        nc.vector.tensor_add(out=both[:], in0=on[:], in1=off[:])
         rboth = keep.tile([V, C], F32)
         nc.vector.reciprocal(out=rboth[:], in_=both[:])
+        prob_avg = keep.tile([V, C], F32)
+        nc.scalar.activation(out=prob_avg[:], in_=q_exp[:], func=ACT.Copy, scale=q_rsum[:, 0:1])
+        nc.sync.dma_start(out=out_0, in_=prob_avg[:])
         mask = keep.tile([V, C], F32)
         nc.vector.tensor_mul(out=mask[:], in0=on[:], in1=rboth[:])
         nc.sync.dma_start(out=out_1, in_=mask[:])

@@ -11,7 +11,6 @@ I32 = mybir.dt.int32
 FP8X4 = mybir.dt.float8_e4m3fn_x4
 ACT = mybir.ActivationFunctionType
 ALU = mybir.AluOpType
-AX = mybir.AxisListType
 
 B, S, V, C, D = 4, 1024, 32, 128, 1024
 P = 128
@@ -20,9 +19,7 @@ PAIR = 2
 PASSES = S // (P * PACK)
 ROWS = B * V
 CHUNKS = D // P
-LOAD_CHUNKS = 2
-ROUNDS = CHUNKS // LOAD_CHUNKS
-WARM_PASSES = 32
+SLOT = 64
 
 EPS_SINK = 0.05
 EPS_LOG = 1e-10
@@ -35,47 +32,44 @@ def tile_cluster_assigner_pa_s_kernel(tc, x, cluster_emb, W, b, noise, out_0, ou
     nc = tc.nc
     with ExitStack() as ctx:
         keep = ctx.enter_context(tc.tile_pool(name="keep", bufs=1))
-        stage = ctx.enter_context(tc.tile_pool(name="stage", bufs=2))
-        psum_t = ctx.enter_context(tc.psum_pool(name="psum_t", bufs=4))
-        psum_e = ctx.enter_context(tc.psum_pool(name="psum_e", bufs=2))
-        psum_s = ctx.enter_context(tc.psum_pool(name="psum_s", bufs=2))
+        stage = ctx.enter_context(tc.tile_pool(name="stage", bufs=3))
+        psum_t = ctx.enter_context(tc.psum_pool(name="psum_t", bufs=3))
+        psum_e = ctx.enter_context(tc.psum_pool(name="psum_e", bufs=4))
+        psum_s = ctx.enter_context(tc.psum_pool(name="psum_s", bufs=1))
 
         ctx.enter_context(tc.manual_schedule())
 
-        ce_raw = keep.tile([C, D], BF16)
-        nc.sync.dma_start(out=ce_raw[:], in_=cluster_emb)
+        bias_raw = keep.tile([P, CHUNKS], BF16)
+        nc.scalar.dma_start(out=bias_raw[:], in_=b.rearrange("(m j) -> m j", j=CHUNKS))
+        noise_raw = keep.tile([V, C], BF16)
+        nc.scalar.dma_start(out=noise_raw[:], in_=noise)
+        w_raw = keep.tile([P, CHUNKS, S], BF16)
+        w_rows = W.rearrange("(m j) t -> m j t", j=CHUNKS)
+
+        def load_w(first, end):
+            nc.sync.dma_start(out=w_raw[:, first:end, :], in_=w_rows[:, first:end, :])
+
+        load_w(0, 1)
         x_raw = keep.tile([P, B, PASSES, PACK, V], BF16)
         nc.sync.dma_start(
             out=x_raw[:].rearrange("p n g (u e) v -> p (n g u) (e v)", e=PAIR),
             in_=x.rearrange("n (g u p e) v -> p (n g u) (e v)", g=PASSES, p=P, e=PAIR),
         )
-        w_raw = keep.tile([P, CHUNKS, S], BF16)
-        w_rows = W.rearrange("(m j) t -> m j t", j=CHUNKS)
-        for rnd in range(ROUNDS):
-            js = slice(rnd * LOAD_CHUNKS, (rnd + 1) * LOAD_CHUNKS)
-            nc.sync.dma_start(out=w_raw[:, js, :], in_=w_rows[:, js, :])
-        bias_raw = keep.tile([P, CHUNKS], BF16)
-        nc.scalar.dma_start(out=bias_raw[:], in_=b.rearrange("(m j) -> m j", j=CHUNKS))
-        noise_raw = keep.tile([V, C], BF16)
-        nc.scalar.dma_start(out=noise_raw[:], in_=noise)
+        load_w(1, 2)
+        load_w(2, 3)
+        load_w(3, 4)
+        load_w(4, 5)
+        load_w(5, 6)
+        load_w(6, 7)
+        load_w(7, 8)
+        ce_raw = keep.tile([C, D], BF16)
+        nc.sync.dma_start(out=ce_raw[:], in_=cluster_emb)
 
         zeros = keep.tile([P, P * PACK], BF16, align_bytes=64)
         nc.vector.memset(zeros[:].bitcast(I32), 0)
         zero_codes = keep.tile([P, P], U32, align_bytes=64)
         zero_scales = keep.tile([P, P], U8, align_bytes=64)
         nc.vector.quantize_mx(out=zero_codes[:].bitcast(FP8X4), scales=zero_scales[:], in_=zeros[:])
-        warm_ps = psum_e.tile([P, P], F32, tag="emb_ps")
-        for idle_pass in range(WARM_PASSES):
-            nc.tensor.matmul_mx(
-                out=warm_ps[:],
-                lhsT=zero_codes[:].bitcast(FP8X4),
-                lhsT_scale=zero_scales[:],
-                rhs=zero_codes[:].bitcast(FP8X4),
-                rhs_scale=zero_scales[:],
-                start=True,
-                stop=True,
-            )
-
         ident = keep.tile([P, P], F32)
         make_identity(nc, ident[:])
         ones = keep.tile([P, P], F32)
@@ -84,37 +78,159 @@ def tile_cluster_assigner_pa_s_kernel(tc, x, cluster_emb, W, b, noise, out_0, ou
         nc.vector.memset(table_in[:], 1.0)
         table_out = keep.tile([P, 1], F32)
         nc.scalar.activation(out=table_out[:], in_=table_in[:], func=ACT.Abs_reciprocal_sqrt)
-        ident_fold = keep.tile([P, V], F32)
-        nc.vector.tensor_reduce(
-            out=ident_fold[:], in_=ident[:].rearrange("p (n v) -> p v n", n=B), axis=AX.X, op=ALU.add
-        )
-        same_v = keep.tile([P, B, V], F32)
-        nc.vector.tensor_copy(out=same_v[:], in_=ident_fold[:].unsqueeze(1).to_broadcast([P, B, V]))
-
-        ce_t = psum_s.tile([P, CHUNKS // PAIR, C], F32, tag="small")
-        ce_words = ce_raw[:].bitcast(F32).rearrange("c (m w) -> c w m", w=CHUNKS // PAIR)
-        for w in range(CHUNKS // PAIR):
-            nc.tensor.transpose(ce_t[:, w, :], ce_words[:, w, :], ident[:])
-        ce_sq = keep.tile([C, D], BF16)
-        ce_ss = keep.tile([C, 1], F32)
-        nc.scalar.activation(out=ce_sq[:], in_=ce_raw[:], func=ACT.Square, accum_out=ce_ss[:])
-        ce_rnorm = keep.tile([C, 1], F32)
-        nc.scalar.activation(out=ce_rnorm[:], in_=ce_ss[:], func=ACT.Abs_reciprocal_sqrt)
-        x_grouped = keep.tile([P, PASSES, ROWS, PACK], BF16, align_bytes=64)
+        xn_grouped = keep.tile([P, PASSES, B, SLOT, PACK], BF16, align_bytes=64)
+        nc.vector.memset(xn_grouped[:].rearrange("p g n c i -> p (g n c i)").bitcast(I32), 0)
+        xn_codes = keep.tile([P, PASSES, (B + 1) * SLOT], U32, align_bytes=64)
+        xn_scales = keep.tile([P, PASSES, (B + 1) * SLOT], U8, align_bytes=64)
         for g in range(PASSES):
-            nc.vector.tensor_copy(
+            nc.vector.memset(xn_codes[:, g, B * SLOT :].bitcast(I32), 0)
+            nc.vector.memset(xn_scales[:, g, B * SLOT :].bitcast(I32), 0)
+
+        def idle_passes(count):
+            warm_ps = psum_s.tile([P, P], F32, tag="sums")
+            for idle_pass in range(count):
+                nc.tensor.matmul_mx(
+                    out=warm_ps[:],
+                    lhsT=zero_codes[:].bitcast(FP8X4),
+                    lhsT_scale=zero_scales[:],
+                    rhs=zero_codes[:].bitcast(FP8X4),
+                    rhs_scale=zero_scales[:],
+                    start=True,
+                    stop=True,
+                )
+
+        w_words = w_raw[:].rearrange("m j t -> m (j t)").bitcast(F32)
+        words_per_chunk = S // PAIR
+        emb = keep.tile([P, CHUNKS, ROWS], F32)
+        emb_sq = keep.tile([P, CHUNKS, ROWS], F32)
+        w_grouped = keep.tile([P, CHUNKS, PASSES, P, PACK], BF16, align_bytes=64)
+        w_codes = keep.tile([P, CHUNKS, PASSES, P], U32, align_bytes=64)
+        w_scales = keep.tile([P, CHUNKS, PASSES, P], U8, align_bytes=64)
+        w_t_of = {}
+        emb_ps_of = {}
+
+        def transpose_w(j):
+            w_t = psum_t.tile([P, PACK, P], F32, tag="turned")
+            w_t_of[j] = w_t
+            for a in range(PACK):
+                first = j * words_per_chunk + a * P
+                nc.tensor.transpose(w_t[:, a, :], w_words[:, first : first + P], ident[:])
+
+        def copy_w(j, copy_out):
+            copy_out(
+                out=w_grouped[:, j]
+                .rearrange("p g m i -> p (g m i)")
+                .bitcast(F32)
+                .rearrange("p (g m u) -> p g m u", g=PASSES, u=PAIR),
+                in_=w_t_of[j][:].rearrange("p (g u) m -> p g m u", g=PASSES),
+            )
+
+        def quantise_w(first, end):
+            nc.vector.quantize_mx(
+                out=w_codes[:, first:end].rearrange("p j g m -> p (j g m)").bitcast(FP8X4),
+                scales=w_scales[:, first:end].rearrange("p j g m -> p (j g m)"),
+                in_=w_grouped[:, first:end].rearrange("p j g m i -> p (j g m i)"),
+            )
+
+        def multiply(js):
+            for j in js:
+                emb_ps = psum_e.tile([P, ROWS], F32, tag="product")
+                emb_ps_of[j] = emb_ps[:]
+                for g in range(PASSES):
+                    nc.tensor.matmul_mx(
+                        out=emb_ps[:],
+                        lhsT=w_codes[:, j, g, :].bitcast(FP8X4),
+                        lhsT_scale=w_scales[:, j, g, :],
+                        rhs=x_codes[:, g, :].bitcast(FP8X4),
+                        rhs_scale=x_scales[:, g, :],
+                        start=(g == 0),
+                        stop=(g == PASSES - 1),
+                    )
+
+        def square(j):
+            nc.scalar.activation(
+                out=emb_sq[:, j, :], in_=emb_ps_of[j], func=ACT.Square, bias=bias[:, j : j + 1]
+            )
+
+        def keep_emb(j):
+            nc.scalar.activation(
+                out=emb[:, j, :], in_=emb_ps_of[j], func=ACT.Identity, bias=bias[:, j : j + 1]
+            )
+
+        sq_pair = keep.tile([P, CHUNKS // 2, ROWS], F32)
+
+        def add_squares(j):
+            nc.vector.tensor_add(out=sq_pair[:, j // 2, :], in0=emb_sq[:, j, :], in1=emb_sq[:, j + 1, :])
+
+        def add_to_norms(squares, start, stop):
+            nc.tensor.matmul(out=ss_ps[:], lhsT=ones[:], rhs=squares, start=start, stop=stop)
+
+        copy_s, copy_v = nc.scalar.copy, nc.vector.tensor_copy
+
+        def cluster_norms():
+            ce_sq = keep.tile([C, D], BF16)
+            nc.vector.scalar_tensor_tensor(
+                out=ce_sq[:], in0=ce_raw[:], scalar=1.0, in1=ce_raw[:], op0=ALU.mult, op1=ALU.mult, accum_out=ce_ss[:]
+            )
+
+        def cluster_one_over_norms():
+            nc.scalar.activation(out=ce_rnorm[:], in_=ce_ss[:], func=ACT.Abs_reciprocal_sqrt)
+
+        def scale_clusters():
+            ce_scale = keep.tile([C, 1], F32)
+            nc.vector.tensor_scalar_min(out=ce_scale[:], in0=ce_rnorm[:], scalar1=INV_NORM_CAP)
+            nc.vector.tensor_scalar_mul(out=cn[:], in0=ce_raw[:], scalar1=ce_scale[:, 0:1])
+
+        def transpose_clusters():
+            cn_t = psum_t.tile([P, CHUNKS // PAIR, C], F32, tag="turned")
+            w_t_of["cn"] = cn_t
+            cn_words = cn[:].bitcast(F32).rearrange("c (m w) -> c w m", w=CHUNKS // PAIR)
+            for w in range(CHUNKS // PAIR):
+                nc.tensor.transpose(cn_t[:, w, :], cn_words[:, w, :], ident[:])
+
+        def copy_clusters(copy_out):
+            copy_out(
+                out=cn_grouped[:]
+                .rearrange("m g c i -> m (g c i)")
+                .bitcast(F32)
+                .rearrange("m (g c u) -> m g c u", g=PASSES, u=PAIR),
+                in_=w_t_of["cn"][:].rearrange("m (g u) c -> m g c u", g=PASSES),
+            )
+
+        def quantise_clusters():
+            nc.vector.quantize_mx(
+                out=cn_codes[:].rearrange("p g c -> p (g c)").bitcast(FP8X4),
+                scales=cn_scales[:].rearrange("p g c -> p (g c)"),
+                in_=cn_grouped[:].rearrange("p g c i -> p (g c i)"),
+            )
+
+        ce_ss = keep.tile([C, 1], F32)
+        ce_rnorm = keep.tile([C, 1], F32)
+        cn = keep.tile([C, D], BF16)
+        cn_grouped = keep.tile([P, PASSES, C, PACK], BF16, align_bytes=64)
+        cn_codes = keep.tile([P, PASSES, C], U32, align_bytes=64)
+        cn_scales = keep.tile([P, PASSES, C], U8, align_bytes=64)
+
+        x_grouped = keep.tile([P, PASSES, ROWS, PACK], BF16, align_bytes=64)
+        x_codes = keep.tile([P, PASSES, ROWS], U32, align_bytes=64)
+        x_scales = keep.tile([P, PASSES, ROWS], U8, align_bytes=64)
+
+        def group_x(g, copy_out):
+            copy_out(
                 out=x_grouped[:, g].rearrange("p (n v) i -> p n v i", n=B),
                 in_=x_raw[:, :, g].rearrange("p n i v -> p n v i"),
             )
-        ce_scale = keep.tile([C, 1], F32)
-        nc.vector.tensor_scalar_min(out=ce_scale[:], in0=ce_rnorm[:], scalar1=INV_NORM_CAP)
-        x_codes = keep.tile([P, PASSES, ROWS], U32, align_bytes=64)
-        x_scales = keep.tile([P, PASSES, ROWS], U8, align_bytes=64)
-        nc.vector.quantize_mx(
-            out=x_codes[:].rearrange("p g r -> p (g r)").bitcast(FP8X4),
-            scales=x_scales[:].rearrange("p g r -> p (g r)"),
-            in_=x_grouped[:].rearrange("p g r i -> p (g r i)"),
-        )
+
+        def quantise_x():
+            nc.vector.quantize_mx(
+                out=x_codes[:].rearrange("p g r -> p (g r)").bitcast(FP8X4),
+                scales=x_scales[:].rearrange("p g r -> p (g r)"),
+                in_=x_grouped[:].rearrange("p g r i -> p (g r i)"),
+            )
+
+        rnorm = keep.tile([P, ROWS], F32)
+
+        idle_passes(10)
         bias = keep.tile([P, CHUNKS], F32)
         nc.vector.tensor_copy(out=bias[:], in_=bias_raw[:])
         u_on = keep.tile([V, C], F32)
@@ -131,156 +247,107 @@ def tile_cluster_assigner_pa_s_kernel(tc, x, cluster_emb, W, b, noise, out_0, ou
         )
         u_off_eps = keep.tile([V, C], F32)
         nc.vector.tensor_scalar_add(out=u_off_eps[:], in0=u_off[:], scalar1=EPS_LOG)
-
-        w_words = w_raw[:].rearrange("m j t -> m (j t)").bitcast(F32)
-        words_per_chunk = S // PAIR
-        w_codes = keep.tile([P, CHUNKS, PASSES, P], U32, align_bytes=64)
-        w_scales = keep.tile([P, CHUNKS, PASSES, P], U8, align_bytes=64)
-        emb = keep.tile([P, CHUNKS, ROWS], F32)
-        w_grouped_of = {}
-        emb_ps_of = {}
-        sq_round = keep.tile([P, ROUNDS, ROWS], F32)
-
-        def transpose_w(rnd):
-            w_grouped = stage.tile([P, LOAD_CHUNKS, PASSES, P, PACK], BF16, align_bytes=64)
-            w_grouped_of[rnd] = w_grouped
-            for k in range(LOAD_CHUNKS):
-                j = rnd * LOAD_CHUNKS + k
-                w_t = psum_t.tile([P, PACK, P], F32)
-                for a in range(PACK):
-                    first = j * words_per_chunk + a * P
-                    nc.tensor.transpose(w_t[:, a, :], w_words[:, first : first + P], ident[:])
-                copy_out = nc.scalar.copy if k % 2 == 0 else nc.vector.tensor_copy
-                copy_out(
-                    out=w_grouped[:, k]
-                    .rearrange("p g m i -> p (g m i)")
-                    .bitcast(F32)
-                    .rearrange("p (g m u) -> p g m u", g=PASSES, u=PAIR),
-                    in_=w_t[:].rearrange("p (g u) m -> p g m u", g=PASSES),
-                )
-
-        def quantise_w(rnd):
-            js = slice(rnd * LOAD_CHUNKS, (rnd + 1) * LOAD_CHUNKS)
-            nc.vector.quantize_mx(
-                out=w_codes[:, js].rearrange("p j g m -> p (j g m)").bitcast(FP8X4),
-                scales=w_scales[:, js].rearrange("p j g m -> p (j g m)"),
-                in_=w_grouped_of[rnd][:].rearrange("p j g m i -> p (j g m i)"),
-            )
-
-        def multiply_w_x(rnd):
-            emb_ps = psum_e.tile([P, LOAD_CHUNKS, ROWS], F32)
-            emb_ps_of[rnd] = emb_ps
-            for k in range(LOAD_CHUNKS):
-                j = rnd * LOAD_CHUNKS + k
-                for g in range(PASSES):
-                    nc.tensor.matmul_mx(
-                        out=emb_ps[:, k, :],
-                        lhsT=w_codes[:, j, g, :].bitcast(FP8X4),
-                        lhsT_scale=w_scales[:, j, g, :],
-                        rhs=x_codes[:, g, :].bitcast(FP8X4),
-                        rhs_scale=x_scales[:, g, :],
-                        start=(g == 0),
-                        stop=(g == PASSES - 1),
-                    )
-
-        def add_bias_and_square(rnd):
-            emb_ps = emb_ps_of[rnd]
-            emb_sq = stage.tile([P, LOAD_CHUNKS, ROWS], F32)
-            for k in range(LOAD_CHUNKS):
-                j = rnd * LOAD_CHUNKS + k
-                nc.scalar.activation(
-                    out=emb_sq[:, k, :], in_=emb_ps[:, k, :], func=ACT.Square, bias=bias[:, j : j + 1]
-                )
-            for k in range(LOAD_CHUNKS):
-                j = rnd * LOAD_CHUNKS + k
-                nc.scalar.activation(
-                    out=emb[:, j, :], in_=emb_ps[:, k, :], func=ACT.Identity, bias=bias[:, j : j + 1]
-                )
-            nc.vector.tensor_add(out=sq_round[:, rnd, :], in0=emb_sq[:, 0, :], in1=emb_sq[:, 1, :])
-
-        def add_to_norms(rnd):
-            nc.tensor.matmul(
-                out=ss_ps[:], lhsT=ones[:], rhs=sq_round[:, rnd, :], start=(rnd == 0), stop=(rnd == ROUNDS - 1)
-            )
-
-        def pipeline_step(s):
-            if s < ROUNDS:
-                transpose_w(s)
-                quantise_w(s)
-            if 2 <= s < ROUNDS + 2:
-                multiply_w_x(s - 2)
-            if s >= 3:
-                add_bias_and_square(s - 3)
-
-        pipeline_step(0)
-        scale_ps = psum_s.tile([P, C], F32, tag="small")
-        nc.tensor.matmul(
-            out=scale_ps[:], lhsT=ce_scale[:, 0:1].to_broadcast([C, P]), rhs=ident[:], start=True, stop=True
-        )
-        cn_scale = keep.tile([P, C], F32)
-        nc.scalar.copy(out=cn_scale[:], in_=scale_ps[:])
-        for s in range(1, ROUNDS + 3):
-            pipeline_step(s)
-        ss_ps = psum_s.tile([P, ROWS], F32, tag="small")
-        for rnd in range(ROUNDS - 1):
-            add_to_norms(rnd)
-
-        add_to_norms(ROUNDS - 1)
-
-        cn_grouped = keep.tile([P, PASSES, C, PACK], BF16, align_bytes=64)
-        for g in range(PASSES):
-            nc.vector.tensor_tensor(
-                out=cn_grouped[:, g].rearrange("m c (u e) -> m c u e", e=PAIR),
-                in0=ce_t[:, PAIR * g : PAIR * (g + 1), :].bitcast(BF16).rearrange("m u (c e) -> m c u e", e=PAIR),
-                in1=cn_scale[:].unsqueeze(2).unsqueeze(3).to_broadcast([P, C, PAIR, PAIR]),
-                op=ALU.mult,
-            )
-        cn_codes = keep.tile([P, PASSES, C], U32, align_bytes=64)
-        cn_scales = keep.tile([P, PASSES, C], U8, align_bytes=64)
-        nc.vector.quantize_mx(
-            out=cn_codes[:].rearrange("p g c -> p (g c)").bitcast(FP8X4),
-            scales=cn_scales[:].rearrange("p g c -> p (g c)"),
-            in_=cn_grouped[:].rearrange("p g c i -> p (g c i)"),
-        )
-
-        rnorm = keep.tile([P, ROWS], F32)
+        transpose_w(0)
+        copy_w(0, copy_s)
+        idle_passes(8)
+        group_x(0, copy_v)
+        group_x(1, copy_v)
+        quantise_w(0, 1)
+        quantise_x()
+        transpose_w(1)
+        copy_w(1, copy_s)
+        transpose_w(2)
+        copy_w(2, copy_v)
+        idle_passes(3)
+        quantise_w(1, 2)
+        transpose_w(3)
+        copy_w(3, copy_s)
+        quantise_w(2, 3)
+        multiply((0,))
+        idle_passes(2)
+        square(0)
+        keep_emb(0)
+        transpose_w(4)
+        copy_w(4, copy_v)
+        transpose_w(5)
+        copy_w(5, copy_s)
+        quantise_w(3, 4)
+        multiply((1, 2))
+        square(1)
+        keep_emb(1)
+        square(2)
+        transpose_w(6)
+        quantise_w(4, 5)
+        copy_w(6, copy_v)
+        transpose_w(7)
+        multiply((3,))
+        copy_w(7, copy_s)
+        quantise_w(5, 6)
+        multiply((4,))
+        idle_passes(2)
+        add_squares(0)
+        quantise_w(6, 7)
+        quantise_w(7, 8)
+        keep_emb(2)
+        square(3)
+        keep_emb(3)
+        multiply((5,))
+        ss_ps = psum_s.tile([P, ROWS], F32, tag="sums")
+        add_to_norms(sq_pair[:, 0, :], True, False)
+        multiply((6,))
+        square(4)
+        square(5)
+        add_squares(2)
+        cluster_norms()
+        add_squares(4)
+        add_to_norms(sq_pair[:, 1, :], False, False)
+        multiply((7,))
+        square(6)
+        square(7)
+        cluster_one_over_norms()
+        scale_clusters()
+        add_to_norms(sq_pair[:, 2, :], False, False)
+        add_to_norms(emb_sq[:, 6, :], False, False)
+        add_to_norms(emb_sq[:, 7, :], False, True)
+        transpose_clusters()
+        keep_emb(4)
+        keep_emb(5)
+        keep_emb(6)
+        keep_emb(7)
         nc.scalar.activation(out=rnorm[:], in_=ss_ps[:], func=ACT.Abs_reciprocal_sqrt)
+        copy_clusters(copy_s)
         nc.scalar.activation(out=table_out[:], in_=rnorm[:, 0:1], func=ACT.Exp)
-        xn_grouped = keep.tile([P, PASSES, ROWS, PACK], BF16, align_bytes=64)
+        idle_passes(16)
+
         for g in range(PASSES):
             nc.vector.scalar_tensor_tensor(
-                out=xn_grouped[:, g],
-                in0=rnorm[:].unsqueeze(2).to_broadcast([P, ROWS, PACK]),
+                out=xn_grouped[:, g, :, 0:V, :],
+                in0=rnorm[:].rearrange("m (n v) -> m n v", n=B).unsqueeze(3).to_broadcast([P, B, V, PACK]),
                 scalar=INV_NORM_CAP,
-                in1=emb[:, PACK * g : PACK * (g + 1), :].rearrange("m i r -> m r i"),
+                in1=emb[:, PACK * g : PACK * (g + 1), :].rearrange("m i (n v) -> m n v i", n=B),
                 op0=ALU.min,
                 op1=ALU.mult,
             )
-        xn_codes = keep.tile([P, PASSES, ROWS], U32, align_bytes=64)
-        xn_scales = keep.tile([P, PASSES, ROWS], U8, align_bytes=64)
-        nc.vector.quantize_mx(
-            out=xn_codes[:].rearrange("p g r -> p (g r)").bitcast(FP8X4),
-            scales=xn_scales[:].rearrange("p g r -> p (g r)"),
-            in_=xn_grouped[:].rearrange("p g r i -> p (g r i)"),
-        )
-
-        prob_ps = psum_s.tile([ROWS, C], F32, tag="small")
+        quantise_clusters()
         for g in range(PASSES):
-            nc.tensor.matmul_mx(
-                out=prob_ps[:],
-                lhsT=xn_codes[:, g, :].bitcast(FP8X4),
-                lhsT_scale=xn_scales[:, g, :],
-                rhs=cn_codes[:, g, :].bitcast(FP8X4),
-                rhs_scale=cn_scales[:, g, :],
-                start=(g == 0),
-                stop=(g == PASSES - 1),
+            nc.vector.quantize_mx(
+                out=xn_codes[:, g, 0 : B * SLOT].bitcast(FP8X4),
+                scales=xn_scales[:, g, 0 : B * SLOT],
+                in_=xn_grouped[:, g].rearrange("p n c i -> p (n c i)"),
             )
-        prob = keep.tile([ROWS, C], F32)
-        nc.vector.tensor_copy(out=prob[:], in_=prob_ps[:])
-        batch_sum_ps = psum_s.tile([ROWS, C], F32, tag="small")
-        nc.tensor.matmul(
-            out=batch_sum_ps[:], lhsT=same_v[:].rearrange("p n v -> p (n v)"), rhs=prob[:], start=True, stop=True
-        )
+
+        batch_sum_ps = psum_e.tile([P, C], F32, tag="product")
+        for g in range(PASSES):
+            for n in range(B):
+                nc.tensor.matmul_mx(
+                    out=batch_sum_ps[:],
+                    lhsT=xn_codes[:, g, n * SLOT : n * SLOT + P].bitcast(FP8X4),
+                    lhsT_scale=xn_scales[:, g, n * SLOT : n * SLOT + P],
+                    rhs=cn_codes[:, g, :].bitcast(FP8X4),
+                    rhs_scale=cn_scales[:, g, :],
+                    start=(g == 0 and n == 0),
+                    stop=(g == PASSES - 1 and n == B - 1),
+                )
 
         q_exp = keep.tile([V, C], F32)
         q_sum = keep.tile([V, 1], F32)

@@ -167,14 +167,22 @@ def tile_cluster_assigner_pa_s_kernel(tc, x, cluster_emb, W, b, noise, out_0, ou
 
         copy_s, copy_v = nc.scalar.copy, nc.vector.tensor_copy
 
-        def cluster_norms():
-            ce_sq = keep.tile([C, D], BF16)
+        def square_clusters(part):
+            half = slice(part * D // 2, (part + 1) * D // 2)
             nc.vector.scalar_tensor_tensor(
-                out=ce_sq[:], in0=ce_raw[:], scalar=1.0, in1=ce_raw[:], op0=ALU.mult, op1=ALU.mult, accum_out=ce_ss[:]
+                out=ce_sq[:, half],
+                in0=ce_raw[:, half],
+                scalar=1.0,
+                in1=ce_raw[:, half],
+                op0=ALU.mult,
+                op1=ALU.mult,
+                accum_out=ce_ss[part][:],
             )
 
         def cluster_one_over_norms():
-            nc.scalar.activation(out=ce_rnorm[:], in_=ce_ss[:], func=ACT.Abs_reciprocal_sqrt)
+            nc.scalar.activation(
+                out=ce_rnorm[:], in_=ce_ss[0][:], func=ACT.Abs_reciprocal_sqrt, bias=ce_ss[1][:, 0:1]
+            )
 
         def scale_clusters():
             ce_scale = keep.tile([C, 1], F32)
@@ -204,7 +212,8 @@ def tile_cluster_assigner_pa_s_kernel(tc, x, cluster_emb, W, b, noise, out_0, ou
                 in_=cn_grouped[:].rearrange("p g c i -> p (g c i)"),
             )
 
-        ce_ss = keep.tile([C, 1], F32)
+        ce_sq = keep.tile([C, D], BF16)
+        ce_ss = [keep.tile([C, 1], F32, name="ce_ss%d" % part) for part in (0, 1)]
         ce_rnorm = keep.tile([C, 1], F32)
         cn = keep.tile([C, D], BF16)
         cn_grouped = keep.tile([P, PASSES, C, PACK], BF16, align_bytes=64)
@@ -283,41 +292,41 @@ def tile_cluster_assigner_pa_s_kernel(tc, x, cluster_emb, W, b, noise, out_0, ou
         multiply((3,))
         copy_w(7, copy_s)
         quantise_w(5, 6)
-        multiply((4,))
-        idle_passes(2)
         add_squares(0)
+        multiply((4,))
         quantise_w(6, 7)
         quantise_w(7, 8)
         keep_emb(2)
         square(3)
         keep_emb(3)
-        multiply((5,))
         ss_ps = psum_s.tile([P, ROWS], F32, tag="sums")
-        add_to_norms(sq_pair[:, 0, :], True, False)
+        add_to_norms(emb_sq[:, 2, :], True, False)
+        multiply((5,))
+        add_to_norms(sq_pair[:, 0, :], False, False)
         multiply((6,))
         square(4)
         square(5)
-        add_squares(2)
-        cluster_norms()
+        square_clusters(0)
         add_squares(4)
-        add_to_norms(sq_pair[:, 1, :], False, False)
+        square_clusters(1)
         multiply((7,))
+        add_to_norms(emb_sq[:, 3, :], False, False)
+        add_to_norms(sq_pair[:, 2, :], False, False)
         square(6)
         square(7)
-        cluster_one_over_norms()
-        scale_clusters()
-        add_to_norms(sq_pair[:, 2, :], False, False)
         add_to_norms(emb_sq[:, 6, :], False, False)
         add_to_norms(emb_sq[:, 7, :], False, True)
-        transpose_clusters()
         keep_emb(4)
         keep_emb(5)
+        cluster_one_over_norms()
+        scale_clusters()
+        transpose_clusters()
         keep_emb(6)
         keep_emb(7)
         nc.scalar.activation(out=rnorm[:], in_=ss_ps[:], func=ACT.Abs_reciprocal_sqrt)
         copy_clusters(copy_s)
         nc.scalar.activation(out=table_out[:], in_=rnorm[:, 0:1], func=ACT.Exp)
-        idle_passes(16)
+        idle_passes(12)
 
         for g in range(PASSES):
             nc.vector.scalar_tensor_tensor(
@@ -328,13 +337,17 @@ def tile_cluster_assigner_pa_s_kernel(tc, x, cluster_emb, W, b, noise, out_0, ou
                 op0=ALU.min,
                 op1=ALU.mult,
             )
-        quantise_clusters()
-        for g in range(PASSES):
+        def quantise_xn(g, first, end):
             nc.vector.quantize_mx(
-                out=xn_codes[:, g, 0 : B * SLOT].bitcast(FP8X4),
-                scales=xn_scales[:, g, 0 : B * SLOT],
-                in_=xn_grouped[:, g].rearrange("p n c i -> p (n c i)"),
+                out=xn_codes[:, g, first * SLOT : end * SLOT].bitcast(FP8X4),
+                scales=xn_scales[:, g, first * SLOT : end * SLOT],
+                in_=xn_grouped[:, g, first:end].rearrange("p n c i -> p (n c i)"),
             )
+
+        quantise_xn(0, 0, B)
+        quantise_clusters()
+        quantise_xn(1, 0, B // 2)
+        quantise_xn(1, B // 2, B)
 
         batch_sum_ps = psum_e.tile([P, C], F32, tag="product")
         for g in range(PASSES):

@@ -39,15 +39,17 @@ def tile_cluster_assigner_pa_s_kernel(tc, x, cluster_emb, W, b, noise, out_0, ou
 
         ctx.enter_context(tc.manual_schedule())
 
-        bias_raw = keep.tile([P, CHUNKS], BF16)
-        nc.scalar.dma_start(out=bias_raw[:], in_=b.rearrange("(m j) -> m j", j=CHUNKS))
+        bias_rows = keep.tile([P, PAIR * P], BF16, align_bytes=64)
+        nc.vector.memset(bias_rows[:].bitcast(I32), 0)
+        nc.scalar.dma_start(out=bias_rows[0 : CHUNKS // PAIR, :], in_=b.rearrange("(a w) -> a w", w=PAIR * P))
         noise_raw = keep.tile([V, C], BF16)
         nc.scalar.dma_start(out=noise_raw[:], in_=noise)
         w_raw = keep.tile([P, CHUNKS, S], BF16)
-        w_rows = W.rearrange("(m j) t -> m j t", j=CHUNKS)
+        w_rows = W.rearrange("(a m e) t -> m a e t", m=P, e=PAIR)
 
-        def load_w(first, end):
-            nc.sync.dma_start(out=w_raw[:, first:end, :], in_=w_rows[:, first:end, :])
+        def load_w(first, end, ts=slice(0, S)):
+            a, e = divmod(first, PAIR)
+            nc.sync.dma_start(out=w_raw[:, first:end, ts], in_=w_rows[:, a, e : e + end - first, ts])
 
         load_w(0, 1)
         x_raw = keep.tile([P, B, PASSES, PACK, V], BF16)
@@ -61,7 +63,8 @@ def tile_cluster_assigner_pa_s_kernel(tc, x, cluster_emb, W, b, noise, out_0, ou
         load_w(4, 5)
         load_w(5, 6)
         load_w(6, 7)
-        load_w(7, 8)
+        load_w(7, 8, slice(0 * S // 2, 1 * S // 2))
+        load_w(7, 8, slice(1 * S // 2, 2 * S // 2))
         ce_raw = keep.tile([C, D], BF16)
         nc.sync.dma_start(out=ce_raw[:], in_=cluster_emb)
 
@@ -109,43 +112,48 @@ def tile_cluster_assigner_pa_s_kernel(tc, x, cluster_emb, W, b, noise, out_0, ou
         w_t_of = {}
         emb_ps_of = {}
 
-        def transpose_w(j):
-            w_t = psum_t.tile([P, PACK, P], F32, tag="turned")
-            w_t_of[j] = w_t
-            for a in range(PACK):
-                first = j * words_per_chunk + a * P
-                nc.tensor.transpose(w_t[:, a, :], w_words[:, first : first + P], ident[:])
+        def transpose_w(j, gs=(0, 1)):
+            w_t = psum_t.tile([P, len(gs) * PAIR, P], F32, tag="turned")
+            for g in gs:
+                w_t_of[j, g] = w_t[:, (g - gs[0]) * PAIR : (g - gs[0] + 1) * PAIR, :]
+                for u in range(PAIR):
+                    first = j * words_per_chunk + (g * PAIR + u) * P
+                    nc.tensor.transpose(w_t_of[j, g][:, u, :], w_words[:, first : first + P], ident[:])
+            if len(gs) == PASSES:
+                w_t_of[j] = w_t
 
-        def copy_w(j, copy_out):
+        def copy_w(j, copy_out, gs=(0, 1)):
+            source = w_t_of[j][:].rearrange("p (g u) m -> p g m u", g=PASSES) if len(gs) == PASSES else (
+                w_t_of[j, gs[0]].rearrange("p (g u) m -> p g m u", g=1))
             copy_out(
-                out=w_grouped[:, j]
+                out=w_grouped[:, j, gs[0] : gs[-1] + 1]
                 .rearrange("p g m i -> p (g m i)")
                 .bitcast(F32)
-                .rearrange("p (g m u) -> p g m u", g=PASSES, u=PAIR),
-                in_=w_t_of[j][:].rearrange("p (g u) m -> p g m u", g=PASSES),
+                .rearrange("p (g m u) -> p g m u", g=len(gs), u=PAIR),
+                in_=source,
             )
 
-        def quantise_w(first, end):
+        def quantise_w(j, gs=(0, 1)):
             nc.vector.quantize_mx(
-                out=w_codes[:, first:end].rearrange("p j g m -> p (j g m)").bitcast(FP8X4),
-                scales=w_scales[:, first:end].rearrange("p j g m -> p (j g m)"),
-                in_=w_grouped[:, first:end].rearrange("p j g m i -> p (j g m i)"),
+                out=w_codes[:, j, gs[0] : gs[-1] + 1].rearrange("p g m -> p (g m)").bitcast(FP8X4),
+                scales=w_scales[:, j, gs[0] : gs[-1] + 1].rearrange("p g m -> p (g m)"),
+                in_=w_grouped[:, j, gs[0] : gs[-1] + 1].rearrange("p g m i -> p (g m i)"),
             )
 
-        def multiply(js):
-            for j in js:
+        def multiply(j, gs=(0, 1)):
+            if gs[0] == 0:
                 emb_ps = psum_e.tile([P, ROWS], F32, tag="product")
                 emb_ps_of[j] = emb_ps[:]
-                for g in range(PASSES):
-                    nc.tensor.matmul_mx(
-                        out=emb_ps[:],
-                        lhsT=w_codes[:, j, g, :].bitcast(FP8X4),
-                        lhsT_scale=w_scales[:, j, g, :],
-                        rhs=x_codes[:, g, :].bitcast(FP8X4),
-                        rhs_scale=x_scales[:, g, :],
-                        start=(g == 0),
-                        stop=(g == PASSES - 1),
-                    )
+            for g in gs:
+                nc.tensor.matmul_mx(
+                    out=emb_ps_of[j],
+                    lhsT=w_codes[:, j, g, :].bitcast(FP8X4),
+                    lhsT_scale=w_scales[:, j, g, :],
+                    rhs=x_codes[:, g, :].bitcast(FP8X4),
+                    rhs_scale=x_scales[:, g, :],
+                    start=(g == 0),
+                    stop=(g == PASSES - 1),
+                )
 
         def square(j):
             nc.scalar.activation(
@@ -157,18 +165,21 @@ def tile_cluster_assigner_pa_s_kernel(tc, x, cluster_emb, W, b, noise, out_0, ou
                 out=emb[:, j, :], in_=emb_ps_of[j], func=ACT.Identity, bias=bias[:, j : j + 1]
             )
 
-        sq_pair = keep.tile([P, CHUNKS // 2, ROWS], F32)
+        sq_pair = keep.tile([P, 3, ROWS], F32)
 
-        def add_squares(j):
-            nc.vector.tensor_add(out=sq_pair[:, j // 2, :], in0=emb_sq[:, j, :], in1=emb_sq[:, j + 1, :])
+        def add_squares(j, k, pair):
+            nc.vector.tensor_add(out=sq_pair[:, pair, :], in0=emb_sq[:, j, :], in1=emb_sq[:, k, :])
 
         def add_to_norms(squares, start, stop):
             nc.tensor.matmul(out=ss_ps[:], lhsT=ones[:], rhs=squares, start=start, stop=stop)
 
         copy_s, copy_v = nc.scalar.copy, nc.vector.tensor_copy
 
-        def square_clusters(part):
+        def square_clusters(part, on_scalar=False):
             half = slice(part * D // 2, (part + 1) * D // 2)
+            if on_scalar:
+                nc.scalar.activation(out=ce_sq[:, half], in_=ce_raw[:, half], func=ACT.Square, accum_out=ce_ss[part][:])
+                return
             nc.vector.scalar_tensor_tensor(
                 out=ce_sq[:, half],
                 in0=ce_raw[:, half],
@@ -192,7 +203,7 @@ def tile_cluster_assigner_pa_s_kernel(tc, x, cluster_emb, W, b, noise, out_0, ou
         def transpose_clusters():
             cn_t = psum_t.tile([P, CHUNKS // PAIR, C], F32, tag="turned")
             w_t_of["cn"] = cn_t
-            cn_words = cn[:].bitcast(F32).rearrange("c (m w) -> c w m", w=CHUNKS // PAIR)
+            cn_words = cn[:].bitcast(F32).rearrange("c (w m) -> c w m", m=P)
             for w in range(CHUNKS // PAIR):
                 nc.tensor.transpose(cn_t[:, w, :], cn_words[:, w, :], ident[:])
 
@@ -240,8 +251,13 @@ def tile_cluster_assigner_pa_s_kernel(tc, x, cluster_emb, W, b, noise, out_0, ou
         rnorm = keep.tile([P, ROWS], F32)
 
         idle_passes(10)
+        bias_t = psum_t.tile([P, P], F32, tag="turned")
+        nc.tensor.transpose(bias_t[:], bias_rows[:].bitcast(F32), ident[:])
+        transpose_w(0)
+        idle_passes(8)
+        transpose_w(1)
         bias = keep.tile([P, CHUNKS], F32)
-        nc.vector.tensor_copy(out=bias[:], in_=bias_raw[:])
+        nc.vector.tensor_copy(out=bias[:], in_=bias_t[:, 0 : CHUNKS // PAIR].bitcast(BF16))
         u_on = keep.tile([V, C], F32)
         nc.vector.tensor_copy(out=u_on[:], in_=noise_raw[:])
         u_on_eps = keep.tile([V, C], F32)
@@ -256,77 +272,79 @@ def tile_cluster_assigner_pa_s_kernel(tc, x, cluster_emb, W, b, noise, out_0, ou
         )
         u_off_eps = keep.tile([V, C], F32)
         nc.vector.tensor_scalar_add(out=u_off_eps[:], in0=u_off[:], scalar1=EPS_LOG)
-        transpose_w(0)
-        copy_w(0, copy_s)
-        idle_passes(8)
         group_x(0, copy_v)
         group_x(1, copy_v)
-        quantise_w(0, 1)
-        quantise_x()
-        transpose_w(1)
+        copy_w(0, copy_s)
         copy_w(1, copy_s)
         transpose_w(2)
-        copy_w(2, copy_v)
         idle_passes(3)
-        quantise_w(1, 2)
         transpose_w(3)
+        quantise_w(0)
+        quantise_x()
+        copy_w(2, copy_v)
+        quantise_w(1)
+        quantise_w(2)
         copy_w(3, copy_s)
-        quantise_w(2, 3)
-        multiply((0,))
+        multiply(0)
         idle_passes(2)
+        transpose_w(4)
+        transpose_w(5)
+        multiply(1)
+        multiply(2)
+        transpose_w(6)
+        copy_w(4, copy_v)
+        quantise_w(3)
+        quantise_w(4)
+        copy_w(6, copy_v)
         square(0)
         keep_emb(0)
-        transpose_w(4)
-        copy_w(4, copy_v)
-        transpose_w(5)
         copy_w(5, copy_s)
-        quantise_w(3, 4)
-        multiply((1, 2))
         square(1)
         keep_emb(1)
         square(2)
-        transpose_w(6)
-        quantise_w(4, 5)
-        copy_w(6, copy_v)
-        transpose_w(7)
-        multiply((3,))
-        copy_w(7, copy_s)
-        quantise_w(5, 6)
-        add_squares(0)
-        multiply((4,))
-        quantise_w(6, 7)
-        quantise_w(7, 8)
+        transpose_w(7, (0,))
+        transpose_w(7, (1,))
+        multiply(3)
+        multiply(4)
+        ss_ps = psum_s.tile([P, ROWS], F32, tag="sums")
+        add_to_norms(emb_sq[:, 2, :], True, False)
+        quantise_w(5)
+        add_squares(0, 1, 0)
+        quantise_w(6)
+        copy_w(7, copy_s, (0,))
+        copy_w(7, copy_s, (1,))
         keep_emb(2)
         square(3)
         keep_emb(3)
-        ss_ps = psum_s.tile([P, ROWS], F32, tag="sums")
-        add_to_norms(emb_sq[:, 2, :], True, False)
-        multiply((5,))
-        add_to_norms(sq_pair[:, 0, :], False, False)
-        multiply((6,))
         square(4)
-        square(5)
+        multiply(5)
+        add_to_norms(sq_pair[:, 0, :], False, False)
+        multiply(6)
+        quantise_w(7, (0,))
+        quantise_w(7, (1,))
         square_clusters(0)
-        add_squares(4)
-        square_clusters(1)
-        multiply((7,))
-        add_to_norms(emb_sq[:, 3, :], False, False)
-        add_to_norms(sq_pair[:, 2, :], False, False)
+        square(5)
         square(6)
+        multiply(7, (0,))
+        multiply(7, (1,))
+        add_to_norms(emb_sq[:, 3, :], False, False)
+        add_squares(4, 5, 1)
+        square_clusters(1)
         square(7)
-        add_to_norms(emb_sq[:, 6, :], False, False)
-        add_to_norms(emb_sq[:, 7, :], False, True)
         keep_emb(4)
         keep_emb(5)
         cluster_one_over_norms()
-        scale_clusters()
-        transpose_clusters()
         keep_emb(6)
         keep_emb(7)
+        add_to_norms(sq_pair[:, 1, :], False, False)
+        add_to_norms(emb_sq[:, 6, :], False, False)
+        add_to_norms(emb_sq[:, 7, :], False, True)
+        scale_clusters()
         nc.scalar.activation(out=rnorm[:], in_=ss_ps[:], func=ACT.Abs_reciprocal_sqrt)
+        transpose_clusters()
+        idle_passes(12)
         copy_clusters(copy_s)
         nc.scalar.activation(out=table_out[:], in_=rnorm[:, 0:1], func=ACT.Exp)
-        idle_passes(12)
 
         for g in range(PASSES):
             nc.vector.scalar_tensor_tensor(

@@ -40,7 +40,7 @@ def tile_cluster_assigner_pa_s_kernel(tc, x, cluster_emb, W, b, noise, out_0, ou
         ctx.enter_context(tc.manual_schedule())
 
         bias_rows = keep.tile([P, PAIR * P], BF16, align_bytes=64)
-        nc.vector.memset(bias_rows[:].bitcast(I32), 0)
+        nc.gpsimd.memset(bias_rows[:].bitcast(I32), 0)
         nc.scalar.dma_start(out=bias_rows[0 : CHUNKS // PAIR, :], in_=b.rearrange("(a w) -> a w", w=PAIR * P))
         noise_raw = keep.tile([V, C], BF16)
         nc.scalar.dma_start(out=noise_raw[:], in_=noise)
@@ -251,36 +251,22 @@ def tile_cluster_assigner_pa_s_kernel(tc, x, cluster_emb, W, b, noise, out_0, ou
         rnorm = keep.tile([P, ROWS], F32)
 
         idle_passes(10)
-        bias_t = psum_t.tile([P, P], F32, tag="turned")
-        nc.tensor.transpose(bias_t[:], bias_rows[:].bitcast(F32), ident[:])
         transpose_w(0)
         idle_passes(8)
         transpose_w(1)
-        bias = keep.tile([P, CHUNKS], F32)
-        nc.vector.tensor_copy(out=bias[:], in_=bias_t[:, 0 : CHUNKS // PAIR].bitcast(BF16))
-        u_on = keep.tile([V, C], F32)
-        nc.vector.tensor_copy(out=u_on[:], in_=noise_raw[:])
-        u_on_eps = keep.tile([V, C], F32)
-        nc.vector.tensor_scalar_mul(out=u_on_eps[:], in0=noise_raw[:], scalar1=EPS_LOG)
-        u_diff = keep.tile([V, C], F32)
-        nc.vector.tensor_scalar(
-            out=u_diff[:], in0=noise_raw[:], scalar1=2.0, scalar2=-1.0, op0=ALU.mult, op1=ALU.add
-        )
-        u_off = keep.tile([V, C], F32)
-        nc.vector.tensor_scalar(
-            out=u_off[:], in0=noise_raw[:], scalar1=-1.0, scalar2=1.0, op0=ALU.mult, op1=ALU.add
-        )
-        u_off_eps = keep.tile([V, C], F32)
-        nc.vector.tensor_scalar_add(out=u_off_eps[:], in0=u_off[:], scalar1=EPS_LOG)
+        bias_t = psum_e.tile([P, P], F32, tag="product")
+        nc.tensor.transpose(bias_t[:], bias_rows[:].bitcast(F32), ident[:])
+        transpose_w(2)
+        idle_passes(3)
         group_x(0, copy_v)
         group_x(1, copy_v)
         copy_w(0, copy_s)
         copy_w(1, copy_s)
-        transpose_w(2)
-        idle_passes(3)
         transpose_w(3)
         quantise_w(0)
         quantise_x()
+        bias = keep.tile([P, CHUNKS], F32)
+        nc.vector.tensor_copy(out=bias[:], in_=bias_t[:, 0 : CHUNKS // PAIR].bitcast(BF16))
         copy_w(2, copy_v)
         quantise_w(1)
         quantise_w(2)
@@ -366,6 +352,21 @@ def tile_cluster_assigner_pa_s_kernel(tc, x, cluster_emb, W, b, noise, out_0, ou
         quantise_clusters()
         quantise_xn(1, 0, B // 2)
         quantise_xn(1, B // 2, B)
+
+        u_on = keep.tile([V, C], F32)
+        nc.vector.tensor_copy(out=u_on[:], in_=noise_raw[:])
+        u_on_eps = keep.tile([V, C], F32)
+        nc.vector.tensor_scalar_mul(out=u_on_eps[:], in0=noise_raw[:], scalar1=EPS_LOG)
+        u_diff = keep.tile([V, C], F32)
+        nc.vector.tensor_scalar(
+            out=u_diff[:], in0=noise_raw[:], scalar1=2.0, scalar2=-1.0, op0=ALU.mult, op1=ALU.add
+        )
+        u_off = keep.tile([V, C], F32)
+        nc.vector.tensor_scalar(
+            out=u_off[:], in0=noise_raw[:], scalar1=-1.0, scalar2=1.0, op0=ALU.mult, op1=ALU.add
+        )
+        u_off_eps = keep.tile([V, C], F32)
+        nc.vector.tensor_scalar_add(out=u_off_eps[:], in0=u_off[:], scalar1=EPS_LOG)
 
         batch_sum_ps = psum_e.tile([P, C], F32, tag="product")
         for g in range(PASSES):

from contextlib import ExitStack

import concourse.mybir as mybir
from concourse.masks import make_identity

F32 = mybir.dt.float32
BF16 = mybir.dt.bfloat16
U32 = mybir.dt.uint32
U8 = mybir.dt.uint8
I32 = mybir.dt.int32
FP8X4 = mybir.dt.float8_e4m3fn_x4
ACT = mybir.ActivationFunctionType
ALU = mybir.AluOpType

B, S, V, C, D = 4, 1024, 32, 128, 1024
P = 128
PACK = 4
PAIR = 2
PASSES = S // (P * PACK)
ROWS = B * V
CHUNKS = D // P
SLOT = 64

EPS_SINK = 0.05
EPS_LOG = 1e-10
INV_NORM_CAP = 1e12

FLOPS = 2 * ROWS * S * D + 2 * ROWS * D * C


def tile_cluster_assigner_pa_s_kernel(tc, x, cluster_emb, W, b, noise, out_0, out_1):
    nc = tc.nc
    with ExitStack() as ctx:
        keep = ctx.enter_context(tc.tile_pool(name="keep", bufs=1))
        stage = ctx.enter_context(tc.tile_pool(name="stage", bufs=3))
        psum_t = ctx.enter_context(tc.psum_pool(name="psum_t", bufs=3))
        psum_e = ctx.enter_context(tc.psum_pool(name="psum_e", bufs=4))
        psum_s = ctx.enter_context(tc.psum_pool(name="psum_s", bufs=1))

        ctx.enter_context(tc.manual_schedule())

        bias_rows = keep.tile([P, PAIR * P], BF16, align_bytes=64)
        nc.gpsimd.memset(bias_rows[:].bitcast(I32), 0)
        nc.scalar.dma_start(out=bias_rows[0 : CHUNKS // PAIR, :], in_=b.rearrange("(a w) -> a w", w=PAIR * P))
        noise_raw = keep.tile([V, C], BF16)
        nc.scalar.dma_start(out=noise_raw[:], in_=noise)
        w_raw = keep.tile([P, CHUNKS, S], BF16)
        w_rows = W.rearrange("(a m e) t -> m a e t", m=P, e=PAIR)

        def load_w(first, end, ts=slice(0, S)):
            a, e = divmod(first, PAIR)
            nc.sync.dma_start(out=w_raw[:, first:end, ts], in_=w_rows[:, a, e : e + end - first, ts])

        load_w(0, 1)
        x_raw = keep.tile([P, B, PASSES, PACK, V], BF16)
        nc.sync.dma_start(
            out=x_raw[:].rearrange("p n g (u e) v -> p (n g u) (e v)", e=PAIR),
            in_=x.rearrange("n (g u p e) v -> p (n g u) (e v)", g=PASSES, p=P, e=PAIR),
        )
        load_w(1, 2)
        load_w(2, 3)
        load_w(3, 4)
        load_w(4, 5)
        load_w(5, 6)
        load_w(6, 7)
        load_w(7, 8, slice(0 * S // 2, 1 * S // 2))
        load_w(7, 8, slice(1 * S // 2, 2 * S // 2))
        ce_raw = keep.tile([C, D], BF16)
        nc.sync.dma_start(out=ce_raw[:], in_=cluster_emb)

        zeros = keep.tile([P, P * PACK], BF16, align_bytes=64)
        nc.vector.memset(zeros[:].bitcast(I32), 0)
        zero_codes = keep.tile([P, P], U32, align_bytes=64)
        zero_scales = keep.tile([P, P], U8, align_bytes=64)
        nc.vector.quantize_mx(out=zero_codes[:].bitcast(FP8X4), scales=zero_scales[:], in_=zeros[:])
        ident = keep.tile([P, P], F32)
        make_identity(nc, ident[:])
        ones = keep.tile([P, P], F32)
        nc.vector.memset(ones[:], 1.0)
        table_in = keep.tile([P, 1], F32)
        nc.vector.memset(table_in[:], 1.0)
        table_out = keep.tile([P, 1], F32)
        nc.scalar.activation(out=table_out[:], in_=table_in[:], func=ACT.Abs_reciprocal_sqrt)
        xn_grouped = keep.tile([P, PASSES, B, SLOT, PACK], BF16, align_bytes=64)
        nc.vector.memset(xn_grouped[:].rearrange("p g n c i -> p (g n c i)").bitcast(I32), 0)
        xn_codes = keep.tile([P, PASSES, (B + 1) * SLOT], U32, align_bytes=64)
        xn_scales = keep.tile([P, PASSES, (B + 1) * SLOT], U8, align_bytes=64)
        for g in range(PASSES):
            nc.vector.memset(xn_codes[:, g, B * SLOT :].bitcast(I32), 0)
            nc.vector.memset(xn_scales[:, g, B * SLOT :].bitcast(I32), 0)

        def idle_passes(count):
            warm_ps = psum_s.tile([P, P], F32, tag="sums")
            for idle_pass in range(count):
                nc.tensor.matmul_mx(
                    out=warm_ps[:],
                    lhsT=zero_codes[:].bitcast(FP8X4),
                    lhsT_scale=zero_scales[:],
                    rhs=zero_codes[:].bitcast(FP8X4),
                    rhs_scale=zero_scales[:],
                    start=True,
                    stop=True,
                )

        w_words = w_raw[:].rearrange("m j t -> m (j t)").bitcast(F32)
        words_per_chunk = S // PAIR
        emb = keep.tile([P, CHUNKS, ROWS], F32)
        emb_sq = keep.tile([P, CHUNKS, ROWS], F32)
        w_grouped = keep.tile([P, CHUNKS, PASSES, P, PACK], BF16, align_bytes=64)
        w_codes = keep.tile([P, CHUNKS, PASSES, P], U32, align_bytes=64)
        w_scales = keep.tile([P, CHUNKS, PASSES, P], U8, align_bytes=64)
        w_t_of = {}
        emb_ps_of = {}

        def transpose_w(j, gs=(0, 1)):
            w_t = psum_t.tile([P, len(gs) * PAIR, P], F32, tag="turned")
            for g in gs:
                w_t_of[j, g] = w_t[:, (g - gs[0]) * PAIR : (g - gs[0] + 1) * PAIR, :]
                for u in range(PAIR):
                    first = j * words_per_chunk + (g * PAIR + u) * P
                    nc.tensor.transpose(w_t_of[j, g][:, u, :], w_words[:, first : first + P], ident[:])
            if len(gs) == PASSES:
                w_t_of[j] = w_t

        def copy_w(j, copy_out, gs=(0, 1)):
            source = w_t_of[j][:].rearrange("p (g u) m -> p g m u", g=PASSES) if len(gs) == PASSES else (
                w_t_of[j, gs[0]].rearrange("p (g u) m -> p g m u", g=1))
            copy_out(
                out=w_grouped[:, j, gs[0] : gs[-1] + 1]
                .rearrange("p g m i -> p (g m i)")
                .bitcast(F32)
                .rearrange("p (g m u) -> p g m u", g=len(gs), u=PAIR),
                in_=source,
            )

        def quantise_w(j, gs=(0, 1)):
            nc.vector.quantize_mx(
                out=w_codes[:, j, gs[0] : gs[-1] + 1].rearrange("p g m -> p (g m)").bitcast(FP8X4),
                scales=w_scales[:, j, gs[0] : gs[-1] + 1].rearrange("p g m -> p (g m)"),
                in_=w_grouped[:, j, gs[0] : gs[-1] + 1].rearrange("p g m i -> p (g m i)"),
            )

        def multiply(j, gs=(0, 1)):
            if gs[0] == 0:
                emb_ps = psum_e.tile([P, ROWS], F32, tag="product")
                emb_ps_of[j] = emb_ps[:]
            for g in gs:
                nc.tensor.matmul_mx(
                    out=emb_ps_of[j],
                    lhsT=w_codes[:, j, g, :].bitcast(FP8X4),
                    lhsT_scale=w_scales[:, j, g, :],
                    rhs=x_codes[:, g, :].bitcast(FP8X4),
                    rhs_scale=x_scales[:, g, :],
                    start=(g == 0),
                    stop=(g == PASSES - 1),
                )

        def square(j):
            nc.scalar.activation(
                out=emb_sq[:, j, :], in_=emb_ps_of[j], func=ACT.Square, bias=bias[:, j : j + 1]
            )

        def keep_emb(j):
            nc.scalar.activation(
                out=emb[:, j, :], in_=emb_ps_of[j], func=ACT.Identity, bias=bias[:, j : j + 1]
            )

        sq_pair = keep.tile([P, 3, ROWS], F32)

        def add_squares(j, k, pair):
            nc.vector.tensor_add(out=sq_pair[:, pair, :], in0=emb_sq[:, j, :], in1=emb_sq[:, k, :])

        def add_to_norms(squares, start, stop):
            nc.tensor.matmul(out=ss_ps[:], lhsT=ones[:], rhs=squares, start=start, stop=stop)

        copy_s, copy_v = nc.scalar.copy, nc.vector.tensor_copy

        def square_clusters(part, on_scalar=False):
            half = slice(part * D // 2, (part + 1) * D // 2)
            if on_scalar:
                nc.scalar.activation(out=ce_sq[:, half], in_=ce_raw[:, half], func=ACT.Square, accum_out=ce_ss[part][:])
                return
            nc.vector.scalar_tensor_tensor(
                out=ce_sq[:, half],
                in0=ce_raw[:, half],
                scalar=1.0,
                in1=ce_raw[:, half],
                op0=ALU.mult,
                op1=ALU.mult,
                accum_out=ce_ss[part][:],
            )

        def cluster_one_over_norms():
            nc.scalar.activation(
                out=ce_rnorm[:], in_=ce_ss[0][:], func=ACT.Abs_reciprocal_sqrt, bias=ce_ss[1][:, 0:1]
            )

        def scale_clusters():
            ce_scale = keep.tile([C, 1], F32)
            nc.vector.tensor_scalar_min(out=ce_scale[:], in0=ce_rnorm[:], scalar1=INV_NORM_CAP)
            nc.vector.tensor_scalar_mul(out=cn[:], in0=ce_raw[:], scalar1=ce_scale[:, 0:1])

        def transpose_clusters():
            cn_t = psum_t.tile([P, CHUNKS // PAIR, C], F32, tag="turned")
            w_t_of["cn"] = cn_t
            cn_words = cn[:].bitcast(F32).rearrange("c (w m) -> c w m", m=P)
            for w in range(CHUNKS // PAIR):
                nc.tensor.transpose(cn_t[:, w, :], cn_words[:, w, :], ident[:])

        def copy_clusters(copy_out):
            copy_out(
                out=cn_grouped[:]
                .rearrange("m g c i -> m (g c i)")
                .bitcast(F32)
                .rearrange("m (g c u) -> m g c u", g=PASSES, u=PAIR),
                in_=w_t_of["cn"][:].rearrange("m (g u) c -> m g c u", g=PASSES),
            )

        def quantise_clusters():
            nc.vector.quantize_mx(
                out=cn_codes[:].rearrange("p g c -> p (g c)").bitcast(FP8X4),
                scales=cn_scales[:].rearrange("p g c -> p (g c)"),
                in_=cn_grouped[:].rearrange("p g c i -> p (g c i)"),
            )

        ce_sq = keep.tile([C, D], BF16)
        ce_ss = [keep.tile([C, 1], F32, name="ce_ss%d" % part) for part in (0, 1)]
        ce_rnorm = keep.tile([C, 1], F32)
        cn = keep.tile([C, D], BF16)
        cn_grouped = keep.tile([P, PASSES, C, PACK], BF16, align_bytes=64)
        cn_codes = keep.tile([P, PASSES, C], U32, align_bytes=64)
        cn_scales = keep.tile([P, PASSES, C], U8, align_bytes=64)

        x_grouped = keep.tile([P, PASSES, ROWS, PACK], BF16, align_bytes=64)
        x_codes = keep.tile([P, PASSES, ROWS], U32, align_bytes=64)
        x_scales = keep.tile([P, PASSES, ROWS], U8, align_bytes=64)

        def group_x(g, copy_out):
            copy_out(
                out=x_grouped[:, g].rearrange("p (n v) i -> p n v i", n=B),
                in_=x_raw[:, :, g].rearrange("p n i v -> p n v i"),
            )

        def quantise_x():
            nc.vector.quantize_mx(
                out=x_codes[:].rearrange("p g r -> p (g r)").bitcast(FP8X4),
                scales=x_scales[:].rearrange("p g r -> p (g r)"),
                in_=x_grouped[:].rearrange("p g r i -> p (g r i)"),
            )

        rnorm = keep.tile([P, ROWS], F32)

        idle_passes(10)
        transpose_w(0)
        idle_passes(8)
        transpose_w(1)
        bias_t = psum_e.tile([P, P], F32, tag="product")
        nc.tensor.transpose(bias_t[:], bias_rows[:].bitcast(F32), ident[:])
        transpose_w(2)
        idle_passes(3)
        group_x(0, copy_v)
        group_x(1, copy_v)
        copy_w(0, copy_s)
        copy_w(1, copy_s)
        transpose_w(3)
        quantise_w(0)
        quantise_x()
        bias = keep.tile([P, CHUNKS], F32)
        nc.vector.tensor_copy(out=bias[:], in_=bias_t[:, 0 : CHUNKS // PAIR].bitcast(BF16))
        copy_w(2, copy_v)
        quantise_w(1)
        quantise_w(2)
        copy_w(3, copy_s)
        multiply(0)
        idle_passes(2)
        transpose_w(4)
        transpose_w(5)
        multiply(1)
        multiply(2)
        transpose_w(6)
        copy_w(4, copy_v)
        quantise_w(3)
        quantise_w(4)
        copy_w(6, copy_v)
        square(0)
        keep_emb(0)
        copy_w(5, copy_s)
        square(1)
        keep_emb(1)
        square(2)
        transpose_w(7, (0,))
        transpose_w(7, (1,))
        multiply(3)
        multiply(4)
        ss_ps = psum_s.tile([P, ROWS], F32, tag="sums")
        add_to_norms(emb_sq[:, 2, :], True, False)
        quantise_w(5)
        add_squares(0, 1, 0)
        quantise_w(6)
        copy_w(7, copy_s, (0,))
        copy_w(7, copy_s, (1,))
        keep_emb(2)
        square(3)
        keep_emb(3)
        square(4)
        multiply(5)
        add_to_norms(sq_pair[:, 0, :], False, False)
        multiply(6)
        quantise_w(7, (0,))
        quantise_w(7, (1,))
        square_clusters(0)
        square(5)
        square(6)
        multiply(7, (0,))
        multiply(7, (1,))
        add_to_norms(emb_sq[:, 3, :], False, False)
        add_squares(4, 5, 1)
        square_clusters(1)
        square(7)
        keep_emb(4)
        keep_emb(5)
        cluster_one_over_norms()
        keep_emb(6)
        keep_emb(7)
        add_to_norms(sq_pair[:, 1, :], False, False)
        add_to_norms(emb_sq[:, 6, :], False, False)
        add_to_norms(emb_sq[:, 7, :], False, True)
        scale_clusters()
        nc.scalar.activation(out=rnorm[:], in_=ss_ps[:], func=ACT.Abs_reciprocal_sqrt)
        transpose_clusters()
        idle_passes(12)
        copy_clusters(copy_s)
        nc.scalar.activation(out=table_out[:], in_=rnorm[:, 0:1], func=ACT.Exp)

        for g in range(PASSES):
            nc.vector.scalar_tensor_tensor(
                out=xn_grouped[:, g, :, 0:V, :],
                in0=rnorm[:].rearrange("m (n v) -> m n v", n=B).unsqueeze(3).to_broadcast([P, B, V, PACK]),
                scalar=INV_NORM_CAP,
                in1=emb[:, PACK * g : PACK * (g + 1), :].rearrange("m i (n v) -> m n v i", n=B),
                op0=ALU.min,
                op1=ALU.mult,
            )
        def quantise_xn(g, first, end):
            nc.vector.quantize_mx(
                out=xn_codes[:, g, first * SLOT : end * SLOT].bitcast(FP8X4),
                scales=xn_scales[:, g, first * SLOT : end * SLOT],
                in_=xn_grouped[:, g, first:end].rearrange("p n c i -> p (n c i)"),
            )

        quantise_xn(0, 0, B)
        quantise_clusters()
        quantise_xn(1, 0, B // 2)
        quantise_xn(1, B // 2, B)

        u_on = keep.tile([V, C], F32)
        nc.vector.tensor_copy(out=u_on[:], in_=noise_raw[:])
        u_on_eps = keep.tile([V, C], F32)
        nc.vector.tensor_scalar_mul(out=u_on_eps[:], in0=noise_raw[:], scalar1=EPS_LOG)
        u_diff = keep.tile([V, C], F32)
        nc.vector.tensor_scalar(
            out=u_diff[:], in0=noise_raw[:], scalar1=2.0, scalar2=-1.0, op0=ALU.mult, op1=ALU.add
        )
        u_off = keep.tile([V, C], F32)
        nc.vector.tensor_scalar(
            out=u_off[:], in0=noise_raw[:], scalar1=-1.0, scalar2=1.0, op0=ALU.mult, op1=ALU.add
        )
        u_off_eps = keep.tile([V, C], F32)
        nc.vector.tensor_scalar_add(out=u_off_eps[:], in0=u_off[:], scalar1=EPS_LOG)

        batch_sum_ps = psum_e.tile([P, C], F32, tag="product")
        for g in range(PASSES):
            for n in range(B):
                nc.tensor.matmul_mx(
                    out=batch_sum_ps[:],
                    lhsT=xn_codes[:, g, n * SLOT : n * SLOT + P].bitcast(FP8X4),
                    lhsT_scale=xn_scales[:, g, n * SLOT : n * SLOT + P],
                    rhs=cn_codes[:, g, :].bitcast(FP8X4),
                    rhs_scale=cn_scales[:, g, :],
                    start=(g == 0 and n == 0),
                    stop=(g == PASSES - 1 and n == B - 1),
                )

        q_exp = keep.tile([V, C], F32)
        q_sum = keep.tile([V, 1], F32)
        nc.scalar.activation(
            out=q_exp[:], in_=batch_sum_ps[0:V, :], func=ACT.Exp, scale=1.0 / (B * EPS_SINK), accum_out=q_sum[:]
        )
        q_diff = keep.tile([V, C], F32)
        nc.vector.tensor_mul(out=q_diff[:], in0=q_exp[:], in1=u_diff[:])
        q_on = keep.tile([V, C], F32)
        nc.vector.tensor_mul(out=q_on[:], in0=q_exp[:], in1=u_on[:])
        both = keep.tile([V, C], F32)
        nc.vector.scalar_tensor_tensor(
            out=both[:], in0=u_off_eps[:], scalar=q_sum[:, 0:1], in1=q_diff[:], op0=ALU.mult, op1=ALU.add
        )
        q_rsum = keep.tile([V, 1], F32)
        nc.vector.reciprocal(out=q_rsum[:], in_=q_sum[:])
        on = keep.tile([V, C], F32)
        nc.vector.scalar_tensor_tensor(
            out=on[:], in0=u_on_eps[:], scalar=q_sum[:, 0:1], in1=q_on[:], op0=ALU.mult, op1=ALU.add
        )
        rboth = keep.tile([V, C], F32)
        nc.vector.reciprocal(out=rboth[:], in_=both[:])
        prob_avg = keep.tile([V, C], F32)
        nc.scalar.activation(out=prob_avg[:], in_=q_exp[:], func=ACT.Copy, scale=q_rsum[:, 0:1])
        nc.sync.dma_start(out=out_0, in_=prob_avg[:])
        mask = keep.tile([V, C], F32)
        nc.vector.tensor_mul(out=mask[:], in0=on[:], in1=rboth[:])
        nc.sync.dma_start(out=out_1, in_=mask[:])
